import numpy as np
import ml_dtypes


def mxq(x, axis, fmt="e4m3"):
    dtype, down = {"e4m3": (ml_dtypes.float8_e4m3fn, 7), "e5m2": (ml_dtypes.float8_e5m2, 14)}[fmt]
    v = np.moveaxis(np.asarray(x, np.float32).astype(ml_dtypes.bfloat16).astype(np.float64), axis, -1)
    blocks = v.reshape(v.shape[:-1] + (-1, 32))
    amax = np.abs(blocks).max(-1, keepdims=True)
    byte = np.maximum(np.where(amax > 0, np.frexp(amax)[1] - 1 + 127, 0) - down, 1)
    scale = np.exp2(byte - 127.0)
    codes = (blocks / scale).astype(np.float32).astype(dtype).astype(np.float64)
    return np.moveaxis((codes * scale).reshape(v.shape), -1, axis)


WIDE = False


def mx_kscale(k):
    if not WIDE:
        return np.ones(k)
    levels = np.array([10, -10, 5, -5, 0])
    a = np.random.permutation(np.resize(levels, k // 512 * 4)).reshape(k // 512, 4)
    idx = np.arange(k)
    return np.exp2(a[idx // 512, idx % 128 // 32])


BF16 = ml_dtypes.bfloat16


def bf(x):
    return np.asarray(x, np.float32).astype(BF16)


def f64(x):
    return np.asarray(x).astype(np.float64)


B, I, H, C, S = 4096, 384, 128, 1023, 3
EPSILON = 1e-6
CC = 1 + C
K = I + H


def setup_inputs():
    s = mx_kscale(K)
    t = mx_kscale(CC)
    t = t / t.min()
    return {
        "invariant_input": bf(np.random.standard_normal((B, I)) * s[:I]),
        "equivariant_input": bf(np.random.standard_normal((B, S)) * 0.125 * t[0]),
        "invariant_hidden": bf(np.random.standard_normal((B, H)) * s[I:]),
        "equivariant_hidden": bf(np.random.standard_normal((B, S, C)) * 0.125 * t[1:]),
        "W_left": bf(np.random.standard_normal((CC, H)) * 0.15 / np.sqrt(CC) * t[:, None]),
        "W_right": bf(np.random.standard_normal((CC, H)) * 0.15 / np.sqrt(CC) * t[:, None]),
        "W_ii": bf(np.random.standard_normal((K, H)) * 0.6 / np.sqrt(K) / s[:, None]),
        "b_ii": bf(np.random.standard_normal(H) * 0.3),
    }


def reference(invariant_input, equivariant_input, invariant_hidden, equivariant_hidden, W_left, W_right, W_ii, b_ii):
    eq_comb = np.concatenate([f64(equivariant_input)[..., None], f64(equivariant_hidden)], axis=-1)
    inv_comb = np.concatenate([f64(invariant_input), f64(invariant_hidden)], axis=-1)
    norm = np.sum(eq_comb * eq_comb, axis=-2, keepdims=True) + EPSILON
    xn = mxq(eq_comb / norm, 2, "e4m3")
    left = xn @ mxq(f64(W_left), 0, "e4m3")
    right = xn @ mxq(f64(W_right), 0, "e4m3")
    proj = np.sum(left * right, axis=-2)
    lin = mxq(inv_comb, 1, "e4m3") @ mxq(f64(W_ii), 0, "e4m3")
    return np.tanh(proj + lin + f64(b_ii))

@@ -1,0 +1,343 @@
+from contextlib import ExitStack
+
+import concourse.mybir as mybir
+from concourse.masks import make_identity
+
+F32 = mybir.dt.float32
+BF16 = mybir.dt.bfloat16
+U32 = mybir.dt.uint32
+U8 = mybir.dt.uint8
+FP8X4 = mybir.dt.float8_e4m3fn_x4
+ACT = mybir.ActivationFunctionType
+ALU = mybir.AluOpType
+
+P = 128
+NT = 32
+NJ = 3
+CC = 1024
+H = 128
+EPS = 1e-6
+FLOPS = 2 * 4096 * 3 * 1024 * 256 + 2 * 4096 * 512 * 128
+
+
+def tile_ryeelman_pa_t_kernel(
+    tc,
+    invariant_input,
+    equivariant_input,
+    invariant_hidden,
+    equivariant_hidden,
+    W_left,
+    W_right,
+    W_ii,
+    b_ii,
+    out,
+):
+    nc = tc.nc
+    hid = equivariant_hidden.rearrange("(p t) j c -> p t j c", t=NT)
+    out_v = out.rearrange("(p t) h -> p t h", t=NT)
+    ii_v = invariant_input.rearrange("(p t) k -> p t k", t=NT)
+    ih_v = invariant_hidden.rearrange("(p t) k -> p t k", t=NT)
+
+    with ExitStack() as ctx:
+        ctx.enter_context(tc.manual_schedule())
+        const = ctx.enter_context(tc.tile_pool(name="const", bufs=1))
+        bigp = ctx.enter_context(tc.tile_pool(name="bigp", bufs=5))
+        work = ctx.enter_context(tc.tile_pool(name="work", bufs=2))
+        ps_n = ctx.enter_context(tc.psum_pool(name="ps_n", bufs=3))
+        ps_e = ctx.enter_context(tc.psum_pool(name="ps_e", bufs=3))
+        ps_o = ctx.enter_context(tc.psum_pool(name="ps_o", bufs=1))
+
+        one_t = const.tile([P, 1], F32, name="one_t")
+        nc.vector.memset(one_t[:], 1.0)
+        eps_t = const.tile([P, 1], F32, name="eps_t")
+        nc.vector.tensor_scalar(out=eps_t[:], in0=one_t[:], scalar1=EPS, scalar2=None, op0=ALU.mult)
+        ident = const.tile([P, P], F32, name="ident")
+        make_identity(nc, ident[:])
+
+        inp = const.tile([P, NT * NJ], BF16, name="inp")
+        nc.scalar.dma_start(out=inp[:], in_=equivariant_input.rearrange("(p t) j -> p (t j)", t=NT))
+        hid15 = const.tile([P, NT * NJ, 16], BF16, name="hid15")
+        nc.scalar.dma_start(
+            out=hid15[:, :, 0:15], in_=hid[:, :, :, 0:15].rearrange("p t j c -> p (t j) c")
+        )
+        wraw = const.tile([P, 2, 2, 4, H], BF16, name="wraw")
+        nc.scalar.dma_start(
+            out=wraw[:, 0].rearrange("p g (u e) h -> p (g u) (e h)", u=2),
+            in_=W_left.rearrange("(c q e) h -> q c (e h)", c=4, e=2),
+        )
+        nc.scalar.dma_start(
+            out=wraw[:, 1].rearrange("p g (u e) h -> p (g u) (e h)", u=2),
+            in_=W_right.rearrange("(c q e) h -> q c (e h)", c=4, e=2),
+        )
+        wiraw = const.tile([P, 4, H], BF16, name="wiraw")
+        nc.scalar.dma_start(
+            out=wiraw[:].rearrange("p (u e) h -> p u (e h)", u=2),
+            in_=W_ii.rearrange("(u q e) h -> q u (e h)", u=2, e=2),
+        )
+        bias_bf = const.tile([P, H], BF16, name="bias_bf")
+        nc.scalar.dma_start(out=bias_bf[:], in_=b_ii.partition_broadcast(P))
+        warm = const.tile([P, 1], F32, name="warm")
+        nc.scalar.activation(out=warm[:], in_=eps_t[:], func=ACT.Abs_reciprocal_sqrt)
+
+        blk0 = const.tile([P, NT * NJ, 16], BF16, name="blk0")
+        nc.vector.tensor_copy(out=blk0[:, :, 1:16], in_=hid15[:, :, 0:15])
+        nc.vector.tensor_copy(out=blk0[:, :, 0:1], in_=inp[:].unsqueeze(2))
+
+        inv_all = const.tile([P, NT, 512], BF16, name="inv_all")
+        icodes = const.tile([P, NT * P], U32, name="icodes", align_bytes=64)
+        iscl = const.tile([P, NT * P], U8, name="iscl", align_bytes=64)
+        pre_all = const.tile([P, NT, H], F32, name="pre_all")
+
+        wgrp = const.tile([P, 2, 2 * H, 4], BF16, name="wgrp", align_bytes=64)
+        wcodes = const.tile([P, 2 * 2 * H], U32, name="wcodes", align_bytes=64)
+        wscl = const.tile([P, 2 * 2 * H], U8, name="wscl", align_bytes=64)
+        wigrp = const.tile([P, H, 4], BF16, name="wigrp", align_bytes=64)
+        wicodes = const.tile([P, H], U32, name="wicodes", align_bytes=64)
+        wiscl = const.tile([P, H], U8, name="wiscl", align_bytes=64)
+
+        def prepare_weights():
+            for g in range(2):
+                nc.vector.tensor_copy(
+                    out=wgrp[:, g].rearrange("p (w h) t -> p w h t", w=2),
+                    in_=wraw[:, :, g].rearrange("p w t h -> p w h t"),
+                )
+            nc.vector.tensor_copy(out=wigrp[:], in_=wiraw[:].rearrange("p t h -> p h t"))
+            nc.vector.quantize_mx(
+                out=wcodes[:].bitcast(FP8X4),
+                scales=wscl[:],
+                in_=wgrp[:].rearrange("p g c t -> p (g c t)"),
+            )
+            nc.vector.quantize_mx(
+                out=wicodes[:].bitcast(FP8X4),
+                scales=wiscl[:],
+                in_=wigrp[:].rearrange("p h t -> p (h t)"),
+            )
+
+        big = {}
+        sq = {}
+        n_t = {}
+        recip = {}
+        eq_t = {}
+        grp = {}
+        codes = {}
+        scl = {}
+        acc = {}
+        rs = {}
+        inv_ps = {}
+        inv_g = {}
+
+        def load(t):
+            big[t] = bigp.tile([P, NJ, CC], BF16, name="big")
+            nc.sync.dma_start(out=big[t][:, :, 16:CC], in_=hid[:, t, :, 15 : CC - 1])
+            nc.gpsimd.tensor_copy(out=big[t][:, :, 0:16], in_=blk0[:, NJ * t : NJ * t + NJ, :])
+
+        def load_inv(c):
+            ts = slice(8 * c, 8 * c + 8)
+            nc.sync.dma_start(out=inv_all[:, ts, 0:384], in_=ii_v[:, ts, :])
+            nc.sync.dma_start(out=inv_all[:, ts, 384:512], in_=ih_v[:, ts, :])
+
+        def squares(t):
+            sq[t] = work.tile([P, NJ, 2, 512], F32, name="sq")
+            who = "svgsvv" if t < 2 else "ssgssg"
+            for i, (g, j) in enumerate((g, j) for g in (1, 0) for j in range(NJ)):
+                src = big[t][:, j, 512 * g : 512 * g + 512].rearrange("p (q e) -> p e q", e=2)
+                dst = sq[t][:, j, :, 256 * g : 256 * g + 256]
+                if who[i] == "s":
+                    nc.scalar.activation(out=dst, in_=src, func=ACT.Square)
+                elif who[i] == "v":
+                    nc.vector.tensor_tensor(out=dst, in0=src, in1=src, op=ALU.mult)
+                else:
+                    nc.gpsimd.tensor_tensor(out=dst, in0=src, in1=src, op=ALU.mult)
+
+        def norm_transposes(t):
+            for g in (1, 0):
+                n_t[t, g] = ps_n.tile([P, 512], F32, name="n_t")
+                for r in range(4):
+                    u, e = divmod(r, 2)
+                    for j in range(NJ):
+                        nc.tensor.matmul(
+                            out=n_t[t, g][:, P * r : P * r + P],
+                            lhsT=sq[t][:, j, e, 256 * g + P * u : 256 * g + P * u + P],
+                            rhs=ident[:],
+                            is_transpose=True,
+                            start=(j == 0),
+                            stop=(j == NJ - 1),
+                        )
+
+        def reciprocal(t):
+            n2 = work.tile([P, CC], F32, name="n2")
+            for g in (1, 0):
+                nc.scalar.activation(
+                    out=n2[:, 512 * g : 512 * g + 512].rearrange("p (b r) -> p b r", r=4),
+                    in_=n_t[t, g][:].rearrange("p (r b) -> p b r", r=4),
+                    func=ACT.Abs_reciprocal_sqrt,
+                    bias=eps_t[:, 0:1],
+                )
+            recip[t] = work.tile([P, CC], F32, name="recip")
+            nc.scalar.activation(out=recip[t][:], in_=n2[:], func=ACT.Square)
+
+        def raw_transposes(t):
+            words = big[t][:].bitcast(F32)
+            for j in range(NJ):
+                eq_t[t, j] = ps_e.tile([P, 512], F32, name="eq_t")
+                for g in range(2):
+                    for u in range(2):
+                        nc.tensor.transpose(
+                            out=eq_t[t, j][:, P * (2 * u + g) : P * (2 * u + g) + P],
+                            in_=words[:, j, P * (2 * g + u) : P * (2 * g + u) + P],
+                            identity=ident[:],
+                        )
+
+        def scale(t, j):
+            if j == 0:
+                grp[t] = work.tile([P, NJ, CC], BF16, name="grp", align_bytes=64)
+            nc.vector.tensor_tensor(
+                out=grp[t][:, j, :].rearrange("p (x u e) -> p x u e", u=2, e=2),
+                in0=eq_t[t, j][:].bitcast(BF16).rearrange("p (u x e) -> p x u e", u=2, e=2),
+                in1=recip[t][:].rearrange("p (x u e) -> p x u e", u=2, e=2),
+                op=ALU.mult,
+            )
+
+        def quantise(t, j):
+            if j == 0:
+                codes[t] = work.tile([P, NJ * 256], U32, name="codes", align_bytes=64)
+                scl[t] = work.tile([P, NJ * 256], U8, name="scl", align_bytes=64)
+            cols = slice(256 * j, 256 * j + 256)
+            nc.vector.quantize_mx(
+                out=codes[t][:, cols].bitcast(FP8X4), scales=scl[t][:, cols], in_=grp[t][:, j, :]
+            )
+
+        def inv_transposes(m):
+            inv_ps[m] = ps_n.tile([P, 512], F32, name="n_t")
+            for tt in range(2):
+                words = inv_all[:, 2 * m + tt, :].bitcast(F32)
+                for u in range(2):
+                    nc.tensor.transpose(
+                        out=inv_ps[m][:, P * (2 * u + tt) : P * (2 * u + tt) + P],
+                        in_=words[:, P * u : P * u + P],
+                        identity=ident[:],
+                    )
+
+        def inv_copy(m):
+            inv_g[m] = work.tile([P, 2 * P * 4], BF16, name="inv_g", align_bytes=64)
+            nc.vector.tensor_copy(
+                out=inv_g[m][:].bitcast(F32).rearrange("p (x u) -> p x u", u=2),
+                in_=inv_ps[m][:].rearrange("p (u x) -> p x u", u=2),
+            )
+
+        def inv_quantise(m):
+            cols = slice(256 * m, 256 * m + 256)
+            nc.vector.quantize_mx(
+                out=icodes[:, cols].bitcast(FP8X4), scales=iscl[:, cols], in_=inv_g[m][:]
+            )
+
+        def products(t):
+            acc[t, 0] = ps_o.tile([P, 512], F32, name="acc_l")
+            acc[t, 1] = ps_o.tile([P, 512], F32, name="acc_r")
+            for j in range(NJ):
+                for g in range(2):
+                    rows = slice(256 * j + P * g, 256 * j + P * g + P)
+                    for w in range(2):
+                        wc = slice(256 * g + P * w, 256 * g + P * w + P)
+                        nc.tensor.matmul_mx(
+                            out=acc[t, w][:, P * j : P * j + P],
+                            lhsT=codes[t][:, rows].bitcast(FP8X4),
+                            lhsT_scale=scl[t][:, rows],
+                            rhs=wcodes[:, wc].bitcast(FP8X4),
+                            rhs_scale=wscl[:, wc],
+                            start=(g == 0),
+                            stop=(g == 1),
+                        )
+            rows = slice(P * t, P * t + P)
+            nc.tensor.matmul_mx(
+                out=acc[t, 1][:, 3 * P : 4 * P],
+                lhsT=icodes[:, rows].bitcast(FP8X4),
+                lhsT_scale=iscl[:, rows],
+                rhs=wicodes[:].bitcast(FP8X4),
+                rhs_scale=wiscl[:],
+                start=True,
+                stop=True,
+            )
+
+        def right_out(t):
+            if t % 2 == 0:
+                rs[t // 2] = work.tile([P, 2, 512], F32, name="rs")
+            nc.scalar.copy(out=rs[t // 2][:, t % 2, :], in_=acc[t, 1][:])
+
+        def left_times_right(t):
+            nc.vector.tensor_tensor(
+                out=rs[t // 2][:, t % 2, 0:384],
+                in0=acc[t, 0][:, 0:384],
+                in1=rs[t // 2][:, t % 2, 0:384],
+                op=ALU.mult,
+            )
+
+        def add_up(m):
+            half = work.tile([P, 2, 256], F32, name="half")
+            nc.gpsimd.tensor_tensor(
+                out=half[:], in0=rs[m][:, :, 0:256], in1=rs[m][:, :, 256:512], op=ALU.add
+            )
+            quarter = work.tile([P, 2, H], F32, name="quarter")
+            nc.gpsimd.tensor_tensor(
+                out=quarter[:], in0=half[:, :, 0:H], in1=half[:, :, H : 2 * H], op=ALU.add
+            )
+            nc.gpsimd.tensor_tensor(
+                out=pre_all[:, 2 * m : 2 * m + 2, :],
+                in0=quarter[:],
+                in1=bias_bf[:].unsqueeze(1).to_broadcast([P, 2, H]),
+                op=ALU.add,
+            )
+
+        def finish(t0, t1):
+            nc.scalar.activation(out=pre_all[:, t0:t1, :], in_=pre_all[:, t0:t1, :], func=ACT.Tanh)
+            nc.sync.dma_start(out=out_v[:, t0:t1, :], in_=pre_all[:, t0:t1, :])
+
+        def has(t):
+            return 0 <= t < NT
+
+        for k in range(-5, NT + 1):
+            m = (k + 1) // 2
+            inv_now = k % 2 == 1 and 0 <= m < NT // 2
+            if has(k + 1):
+                reciprocal(k + 1)
+            if has(k - 1):
+                products(k - 1)
+                right_out(k - 1)
+            if k == NT - 1:
+                finish(0, 16)
+                finish(16, 28)
+            if k == NT:
+                finish(28, 30)
+            if inv_now:
+                inv_transposes(m)
+            if k == -1:
+                raw_transposes(0)
+            if has(k):
+                scale(k, 0)
+                scale(k, 1)
+                quantise(k, 0)
+                scale(k, 2)
+                quantise(k, 1)
+            if inv_now:
+                inv_copy(m)
+            if has(k - 1):
+                left_times_right(k - 1)
+            if has(k):
+                quantise(k, 2)
+            if inv_now:
+                inv_quantise(m)
+            if has(k + 2):
+                norm_transposes(k + 2)
+            if has(k + 1) and k != -1:
+                raw_transposes(k + 1)
+            if has(k + 5):
+                load(k + 5)
+            if -4 <= k <= -1:
+                load_inv(k + 4)
+            if has(k + 3):
+                squares(k + 3)
+            if k == -3:
+                prepare_weights()
+            if has(k - 1) and (k - 1) % 2 == 1:
+                add_up((k - 1) // 2)
+        finish(30, 32)

@@ -57,9 +57,14 @@ def tile_ryeelman_pa_t_kernel(
         inp = const.tile([P, NT * NJ], BF16, name="inp")
         nc.scalar.dma_start(out=inp[:], in_=equivariant_input.rearrange("(p t) j -> p (t j)", t=NT))
         hid15 = const.tile([P, NT * NJ, 16], BF16, name="hid15")
-        nc.scalar.dma_start(
-            out=hid15[:, :, 0:15], in_=hid[:, :, :, 0:15].rearrange("p t j c -> p (t j) c")
-        )
+
+        def load_first_channels(t0, t1):
+            nc.scalar.dma_start(
+                out=hid15[:, NJ * t0 : NJ * t1, 0:15],
+                in_=hid[:, t0:t1, :, 0:15].rearrange("p t j c -> p (t j) c"),
+            )
+
+        load_first_channels(0, 4)
         wraw = const.tile([P, 2, 2, 4, H], BF16, name="wraw")
         nc.scalar.dma_start(
             out=wraw[:, 0].rearrange("p g (u e) h -> p (g u) (e h)", u=2),
@@ -76,12 +81,13 @@ def tile_ryeelman_pa_t_kernel(
         )
         bias_bf = const.tile([P, H], BF16, name="bias_bf")
         nc.scalar.dma_start(out=bias_bf[:], in_=b_ii.partition_broadcast(P))
+        load_first_channels(4, NT)
         warm = const.tile([P, 1], F32, name="warm")
         nc.scalar.activation(out=warm[:], in_=eps_t[:], func=ACT.Abs_reciprocal_sqrt)
 
         blk0 = const.tile([P, NT * NJ, 16], BF16, name="blk0")
-        nc.vector.tensor_copy(out=blk0[:, :, 1:16], in_=hid15[:, :, 0:15])
         nc.vector.tensor_copy(out=blk0[:, :, 0:1], in_=inp[:].unsqueeze(2))
+        nc.vector.tensor_copy(out=blk0[:, 0 : NJ * 4, 1:16], in_=hid15[:, 0 : NJ * 4, 0:15])
 
         inv_all = const.tile([P, NT, 512], BF16, name="inv_all")
         icodes = const.tile([P, NT * P], U32, name="icodes", align_bytes=64)
@@ -129,7 +135,9 @@ def tile_ryeelman_pa_t_kernel(
         def load(t):
             big[t] = bigp.tile([P, NJ, CC], BF16, name="big")
             nc.sync.dma_start(out=big[t][:, :, 16:CC], in_=hid[:, t, :, 15 : CC - 1])
-            nc.gpsimd.tensor_copy(out=big[t][:, :, 0:16], in_=blk0[:, NJ * t : NJ * t + NJ, :])
+
+        def first_channels(t):
+            nc.scalar.copy(out=big[t][:, :, 0:16], in_=blk0[:, NJ * t : NJ * t + NJ, :])
 
         def load_inv(c):
             ts = slice(8 * c, 8 * c + 8)
@@ -138,7 +146,7 @@ def tile_ryeelman_pa_t_kernel(
 
         def squares(t):
             sq[t] = work.tile([P, NJ, 2, 512], F32, name="sq")
-            who = "svgsvv" if t < 2 else "ssgssg"
+            who = "svssvg" if t < 2 else ("svsssg" if t % 2 == 1 else "sssssg")
             for i, (g, j) in enumerate((g, j) for g in (1, 0) for j in range(NJ)):
                 src = big[t][:, j, 512 * g : 512 * g + 512].rearrange("p (q e) -> p e q", e=2)
                 dst = sq[t][:, j, :, 256 * g : 256 * g + 256]
@@ -149,19 +157,25 @@ def tile_ryeelman_pa_t_kernel(
                 else:
                     nc.gpsimd.tensor_tensor(out=dst, in0=src, in1=src, op=ALU.mult)
 
+        def pre_add(t, g, eng):
+            cols = slice(256 * g, 256 * g + 256)
+            eng.tensor_tensor(
+                out=sq[t][:, 0, :, cols], in0=sq[t][:, 0, :, cols], in1=sq[t][:, 1, :, cols], op=ALU.add
+            )
+
         def norm_transposes(t):
             for g in (1, 0):
                 n_t[t, g] = ps_n.tile([P, 512], F32, name="n_t")
                 for r in range(4):
                     u, e = divmod(r, 2)
-                    for j in range(NJ):
+                    for j in (0, 2):
                         nc.tensor.matmul(
                             out=n_t[t, g][:, P * r : P * r + P],
                             lhsT=sq[t][:, j, e, 256 * g + P * u : 256 * g + P * u + P],
                             rhs=ident[:],
                             is_transpose=True,
                             start=(j == 0),
-                            stop=(j == NJ - 1),
+                            stop=(j == 2),
                         )
 
         def reciprocal(t):
@@ -272,16 +286,16 @@ def tile_ryeelman_pa_t_kernel(
                 op=ALU.mult,
             )
 
-        def add_up(m):
+        def add_up(m, eng):
             half = work.tile([P, 2, 256], F32, name="half")
-            nc.gpsimd.tensor_tensor(
+            eng.tensor_tensor(
                 out=half[:], in0=rs[m][:, :, 0:256], in1=rs[m][:, :, 256:512], op=ALU.add
             )
             quarter = work.tile([P, 2, H], F32, name="quarter")
-            nc.gpsimd.tensor_tensor(
+            eng.tensor_tensor(
                 out=quarter[:], in0=half[:, :, 0:H], in1=half[:, :, H : 2 * H], op=ALU.add
             )
-            nc.gpsimd.tensor_tensor(
+            eng.tensor_tensor(
                 out=pre_all[:, 2 * m : 2 * m + 2, :],
                 in0=quarter[:],
                 in1=bias_bf[:].unsqueeze(1).to_broadcast([P, 2, H]),
@@ -312,6 +326,11 @@ def tile_ryeelman_pa_t_kernel(
                 inv_transposes(m)
             if k == -1:
                 raw_transposes(0)
+            if has(k + 2):
+                pre_add(k + 2, 1, nc.vector if k + 2 < 2 else nc.gpsimd)
+                pre_add(k + 2, 0, nc.vector if k + 2 < 2 else nc.gpsimd)
+            if k == -1:
+                prepare_weights()
             if has(k):
                 scale(k, 0)
                 scale(k, 1)
@@ -326,6 +345,8 @@ def tile_ryeelman_pa_t_kernel(
                 quantise(k, 2)
             if inv_now:
                 inv_quantise(m)
+            if k == 0:
+                nc.vector.tensor_copy(out=blk0[:, NJ * 4 :, 1:16], in_=hid15[:, NJ * 4 :, 0:15])
             if has(k + 2):
                 norm_transposes(k + 2)
             if has(k + 1) and k != -1:
@@ -336,8 +357,8 @@ def tile_ryeelman_pa_t_kernel(
                 load_inv(k + 4)
             if has(k + 3):
                 squares(k + 3)
-            if k == -3:
-                prepare_weights()
+            if has(k + 4):
+                first_channels(k + 4)
             if has(k - 1) and (k - 1) % 2 == 1:
-                add_up((k - 1) // 2)
+                add_up((k - 1) // 2, nc.vector if k == NT else nc.gpsimd)
         finish(30, 32)

@@ -157,18 +157,12 @@ def tile_ryeelman_pa_t_kernel(
                 else:
                     nc.gpsimd.tensor_tensor(out=dst, in0=src, in1=src, op=ALU.mult)
 
-        def pre_add(t, g, eng):
-            cols = slice(256 * g, 256 * g + 256)
-            eng.tensor_tensor(
-                out=sq[t][:, 0, :, cols], in0=sq[t][:, 0, :, cols], in1=sq[t][:, 1, :, cols], op=ALU.add
-            )
-
         def norm_transposes(t):
             for g in (1, 0):
                 n_t[t, g] = ps_n.tile([P, 512], F32, name="n_t")
                 for r in range(4):
                     u, e = divmod(r, 2)
-                    for j in (0, 2):
+                    for j in range(NJ):
                         nc.tensor.matmul(
                             out=n_t[t, g][:, P * r : P * r + P],
                             lhsT=sq[t][:, j, e, 256 * g + P * u : 256 * g + P * u + P],
@@ -326,9 +320,6 @@ def tile_ryeelman_pa_t_kernel(
                 inv_transposes(m)
             if k == -1:
                 raw_transposes(0)
-            if has(k + 2):
-                pre_add(k + 2, 1, nc.vector if k + 2 < 2 else nc.gpsimd)
-                pre_add(k + 2, 0, nc.vector if k + 2 < 2 else nc.gpsimd)
             if k == -1:
                 prepare_weights()
             if has(k):

@@ -146,7 +146,7 @@ def tile_ryeelman_pa_t_kernel(
 
         def squares(t):
             sq[t] = work.tile([P, NJ, 2, 512], F32, name="sq")
-            who = "svssvg" if t < 2 else ("svsssg" if t % 2 == 1 else "sssssg")
+            who = "svssvg" if t < 2 else "sssssg"
             for i, (g, j) in enumerate((g, j) for g in (1, 0) for j in range(NJ)):
                 src = big[t][:, j, 512 * g : 512 * g + 512].rearrange("p (q e) -> p e q", e=2)
                 dst = sq[t][:, j, :, 256 * g : 256 * g + 256]
@@ -157,12 +157,20 @@ def tile_ryeelman_pa_t_kernel(
                 else:
                     nc.gpsimd.tensor_tensor(out=dst, in0=src, in1=src, op=ALU.mult)
 
+        def pre_add(t):
+            nc.vector.tensor_tensor(
+                out=sq[t][:, 0, :, 256:512],
+                in0=sq[t][:, 0, :, 256:512],
+                in1=sq[t][:, 1, :, 256:512],
+                op=ALU.add,
+            )
+
         def norm_transposes(t):
             for g in (1, 0):
                 n_t[t, g] = ps_n.tile([P, 512], F32, name="n_t")
                 for r in range(4):
                     u, e = divmod(r, 2)
-                    for j in range(NJ):
+                    for j in (0, 2) if g == 1 else (0, 1, 2):
                         nc.tensor.matmul(
                             out=n_t[t, g][:, P * r : P * r + P],
                             lhsT=sq[t][:, j, e, 256 * g + P * u : 256 * g + P * u + P],
@@ -228,7 +236,7 @@ def tile_ryeelman_pa_t_kernel(
 
         def inv_copy(m):
             inv_g[m] = work.tile([P, 2 * P * 4], BF16, name="inv_g", align_bytes=64)
-            nc.vector.tensor_copy(
+            nc.scalar.copy(
                 out=inv_g[m][:].bitcast(F32).rearrange("p (x u) -> p x u", u=2),
                 in_=inv_ps[m][:].rearrange("p (u x) -> p x u", u=2),
             )
@@ -320,6 +328,8 @@ def tile_ryeelman_pa_t_kernel(
                 inv_transposes(m)
             if k == -1:
                 raw_transposes(0)
+            if has(k + 2):
+                pre_add(k + 2)
             if k == -1:
                 prepare_weights()
             if has(k):

@@ -146,31 +146,26 @@ def tile_ryeelman_pa_t_kernel(
 
         def squares(t):
             sq[t] = work.tile([P, NJ, 2, 512], F32, name="sq")
-            who = "svssvg" if t < 2 else "sssssg"
-            for i, (g, j) in enumerate((g, j) for g in (1, 0) for j in range(NJ)):
-                src = big[t][:, j, 512 * g : 512 * g + 512].rearrange("p (q e) -> p e q", e=2)
-                dst = sq[t][:, j, :, 256 * g : 256 * g + 256]
-                if who[i] == "s":
+            if t < 2:
+                plan = (("s", 0, 0, 512), ("v", 1, 0, 512), ("s", 2, 0, 256), ("v", 2, 256, 512))
+            else:
+                plan = (("s", 0, 0, 512), ("s", 1, 0, 512), ("g", 2, 0, 512))
+            for who, j, q0, q1 in plan:
+                src = big[t][:, j, 2 * q0 : 2 * q1].rearrange("p (q e) -> p e q", e=2)
+                dst = sq[t][:, j, :, q0:q1]
+                if who == "s":
                     nc.scalar.activation(out=dst, in_=src, func=ACT.Square)
-                elif who[i] == "v":
+                elif who == "v":
                     nc.vector.tensor_tensor(out=dst, in0=src, in1=src, op=ALU.mult)
                 else:
                     nc.gpsimd.tensor_tensor(out=dst, in0=src, in1=src, op=ALU.mult)
-
-        def pre_add(t):
-            nc.vector.tensor_tensor(
-                out=sq[t][:, 0, :, 256:512],
-                in0=sq[t][:, 0, :, 256:512],
-                in1=sq[t][:, 1, :, 256:512],
-                op=ALU.add,
-            )
 
         def norm_transposes(t):
             for g in (1, 0):
                 n_t[t, g] = ps_n.tile([P, 512], F32, name="n_t")
                 for r in range(4):
                     u, e = divmod(r, 2)
-                    for j in (0, 2) if g == 1 else (0, 1, 2):
+                    for j in range(NJ):
                         nc.tensor.matmul(
                             out=n_t[t, g][:, P * r : P * r + P],
                             lhsT=sq[t][:, j, e, 256 * g + P * u : 256 * g + P * u + P],
@@ -214,14 +209,16 @@ def tile_ryeelman_pa_t_kernel(
                 op=ALU.mult,
             )
 
-        def quantise(t, j):
-            if j == 0:
-                codes[t] = work.tile([P, NJ * 256], U32, name="codes", align_bytes=64)
-                scl[t] = work.tile([P, NJ * 256], U8, name="scl", align_bytes=64)
-            cols = slice(256 * j, 256 * j + 256)
-            nc.vector.quantize_mx(
-                out=codes[t][:, cols].bitcast(FP8X4), scales=scl[t][:, cols], in_=grp[t][:, j, :]
-            )
+        def quantise(t):
+            codes[t] = work.tile([P, NJ * 256], U32, name="codes", align_bytes=64)
+            scl[t] = work.tile([P, NJ * 256], U8, name="scl", align_bytes=64)
+            flat = grp[t][:].rearrange("p j c -> p (j c)")
+            for w0, w1 in ((0, 512), (512, 768)):
+                nc.vector.quantize_mx(
+                    out=codes[t][:, w0:w1].bitcast(FP8X4),
+                    scales=scl[t][:, w0:w1],
+                    in_=flat[:, 4 * w0 : 4 * w1],
+                )
 
         def inv_transposes(m):
             inv_ps[m] = ps_n.tile([P, 512], F32, name="n_t")
@@ -328,22 +325,18 @@ def tile_ryeelman_pa_t_kernel(
                 inv_transposes(m)
             if k == -1:
                 raw_transposes(0)
-            if has(k + 2):
-                pre_add(k + 2)
             if k == -1:
                 prepare_weights()
+            if inv_now:
+                inv_copy(m)
             if has(k):
                 scale(k, 0)
                 scale(k, 1)
-                quantise(k, 0)
                 scale(k, 2)
-                quantise(k, 1)
-            if inv_now:
-                inv_copy(m)
             if has(k - 1):
                 left_times_right(k - 1)
             if has(k):
-                quantise(k, 2)
+                quantise(k)
             if inv_now:
                 inv_quantise(m)
             if k == 0:

@@ -149,7 +149,14 @@ def tile_ryeelman_pa_t_kernel(
             if t < 2:
                 plan = (("s", 0, 0, 512), ("v", 1, 0, 512), ("s", 2, 0, 256), ("v", 2, 256, 512))
             else:
-                plan = (("s", 0, 0, 512), ("s", 1, 0, 512), ("g", 2, 0, 512))
+                plan = (
+                    ("s", 0, 0, 512),
+                    ("s", 1, 0, 512),
+                    ("g", 2, 0, 128),
+                    ("g", 2, 128, 256),
+                    ("g", 2, 256, 384),
+                    ("g", 2, 384, 512),
+                )
             for who, j, q0, q1 in plan:
                 src = big[t][:, j, 2 * q0 : 2 * q1].rearrange("p (q e) -> p e q", e=2)
                 dst = sq[t][:, j, :, q0:q1]

@@ -20,6 +20,10 @@ EPS = 1e-6
 FLOPS = 2 * 4096 * 3 * 1024 * 256 + 2 * 4096 * 512 * 128
 
 
+def row(t):
+    return NT - 1 - t
+
+
 def tile_ryeelman_pa_t_kernel(
     tc,
     invariant_input,
@@ -49,50 +53,58 @@ def tile_ryeelman_pa_t_kernel(
 
         one_t = const.tile([P, 1], F32, name="one_t")
         nc.vector.memset(one_t[:], 1.0)
+        warm = const.tile([P, 1], F32, name="warm")
+        nc.scalar.activation(out=warm[:], in_=one_t[:], func=ACT.Abs_reciprocal_sqrt)
         eps_t = const.tile([P, 1], F32, name="eps_t")
         nc.vector.tensor_scalar(out=eps_t[:], in0=one_t[:], scalar1=EPS, scalar2=None, op0=ALU.mult)
         ident = const.tile([P, P], F32, name="ident")
         make_identity(nc, ident[:])
 
         inp = const.tile([P, NT * NJ], BF16, name="inp")
-        nc.scalar.dma_start(out=inp[:], in_=equivariant_input.rearrange("(p t) j -> p (t j)", t=NT))
+        nc.sync.dma_start(out=inp[:], in_=equivariant_input.rearrange("(p t) j -> p (t j)", t=NT))
         hid15 = const.tile([P, NT * NJ, 16], BF16, name="hid15")
 
-        def load_first_channels(t0, t1):
-            nc.scalar.dma_start(
-                out=hid15[:, NJ * t0 : NJ * t1, 0:15],
-                in_=hid[:, t0:t1, :, 0:15].rearrange("p t j c -> p (t j) c"),
+        def load_first_channels(q0, q1):
+            nc.sync.dma_start(
+                out=hid15[:, NJ * q0 : NJ * q1, 0:15],
+                in_=hid[:, q0:q1, :, 0:15].rearrange("p t j c -> p (t j) c"),
             )
 
-        load_first_channels(0, 4)
+        load_first_channels(NT - 4, NT)
         wraw = const.tile([P, 2, 2, 4, H], BF16, name="wraw")
-        nc.scalar.dma_start(
-            out=wraw[:, 0].rearrange("p g (u e) h -> p (g u) (e h)", u=2),
-            in_=W_left.rearrange("(c q e) h -> q c (e h)", c=4, e=2),
-        )
-        nc.scalar.dma_start(
-            out=wraw[:, 1].rearrange("p g (u e) h -> p (g u) (e h)", u=2),
-            in_=W_right.rearrange("(c q e) h -> q c (e h)", c=4, e=2),
-        )
         wiraw = const.tile([P, 4, H], BF16, name="wiraw")
-        nc.scalar.dma_start(
-            out=wiraw[:].rearrange("p (u e) h -> p u (e h)", u=2),
-            in_=W_ii.rearrange("(u q e) h -> q u (e h)", u=2, e=2),
-        )
         bias_bf = const.tile([P, H], BF16, name="bias_bf")
-        nc.scalar.dma_start(out=bias_bf[:], in_=b_ii.partition_broadcast(P))
-        load_first_channels(4, NT)
-        warm = const.tile([P, 1], F32, name="warm")
-        nc.scalar.activation(out=warm[:], in_=eps_t[:], func=ACT.Abs_reciprocal_sqrt)
+
+        def load_weights():
+            for w, weights in ((0, W_left), (1, W_right)):
+                nc.sync.dma_start(
+                    out=wraw[:, w].rearrange("p g (u e) h -> p (g u) (e h)", u=2),
+                    in_=weights.rearrange("(c q e) h -> q c (e h)", c=4, e=2),
+                )
+            nc.sync.dma_start(
+                out=wiraw[:].rearrange("p (u e) h -> p u (e h)", u=2),
+                in_=W_ii.rearrange("(u q e) h -> q u (e h)", u=2, e=2),
+            )
+            nc.sync.dma_start(out=bias_bf[:], in_=b_ii.partition_broadcast(P))
 
         blk0 = const.tile([P, NT * NJ, 16], BF16, name="blk0")
         nc.vector.tensor_copy(out=blk0[:, :, 0:1], in_=inp[:].unsqueeze(2))
-        nc.vector.tensor_copy(out=blk0[:, 0 : NJ * 4, 1:16], in_=hid15[:, 0 : NJ * 4, 0:15])
+
+        def place_first_channels(q0, q1):
+            rows = slice(NJ * q0, NJ * q1)
+            nc.vector.tensor_copy(out=blk0[:, rows, 1:16], in_=hid15[:, rows, 0:15])
+
+        place_first_channels(NT - 4, NT)
 
         inv_all = const.tile([P, NT, 512], BF16, name="inv_all")
         icodes = const.tile([P, NT * P], U32, name="icodes", align_bytes=64)
         iscl = const.tile([P, NT * P], U8, name="iscl", align_bytes=64)
-        pre_all = const.tile([P, NT, H], F32, name="pre_all")
+        prod = const.tile([P, 3 * H + NT * H], F32, name="prod")
+        rr = const.tile([P, 3, 5 * H], F32, name="rr")
+        for i in range(3):
+            nc.vector.memset(rr[:, i, 4 * H : 5 * H], 1.0)
+        bias_f = const.tile([P, H], F32, name="bias_f")
+        bias_t = const.tile([P, P], F32, name="bias_t")
 
         wgrp = const.tile([P, 2, 2 * H, 4], BF16, name="wgrp", align_bytes=64)
         wcodes = const.tile([P, 2 * 2 * H], U32, name="wcodes", align_bytes=64)
@@ -119,6 +131,12 @@ def tile_ryeelman_pa_t_kernel(
                 in_=wigrp[:].rearrange("p h t -> p (h t)"),
             )
 
+        def prepare_bias():
+            nc.vector.tensor_copy(out=bias_f[:], in_=bias_bf[:])
+            ps = ps_o.tile([P, 512], F32, name="acc_l")
+            nc.tensor.transpose(out=ps[:, 0:P], in_=bias_f[:], identity=ident[:])
+            nc.vector.tensor_copy(out=bias_t[:], in_=ps[:, 0:P])
+
         big = {}
         sq = {}
         n_t = {}
@@ -128,19 +146,19 @@ def tile_ryeelman_pa_t_kernel(
         codes = {}
         scl = {}
         acc = {}
-        rs = {}
         inv_ps = {}
         inv_g = {}
 
         def load(t):
             big[t] = bigp.tile([P, NJ, CC], BF16, name="big")
-            nc.sync.dma_start(out=big[t][:, :, 16:CC], in_=hid[:, t, :, 15 : CC - 1])
+            nc.sync.dma_start(out=big[t][:, :, 16:CC], in_=hid[:, row(t), :, 15 : CC - 1])
 
         def first_channels(t):
-            nc.scalar.copy(out=big[t][:, :, 0:16], in_=blk0[:, NJ * t : NJ * t + NJ, :])
+            q = row(t)
+            nc.scalar.copy(out=big[t][:, :, 0:16], in_=blk0[:, NJ * q : NJ * q + NJ, :])
 
         def load_inv(c):
-            ts = slice(8 * c, 8 * c + 8)
+            ts = slice(NT - 8 * c - 8, NT - 8 * c)
             nc.sync.dma_start(out=inv_all[:, ts, 0:384], in_=ii_v[:, ts, :])
             nc.sync.dma_start(out=inv_all[:, ts, 384:512], in_=ih_v[:, ts, :])
 
@@ -151,7 +169,9 @@ def tile_ryeelman_pa_t_kernel(
             else:
                 plan = (
                     ("s", 0, 0, 512),
-                    ("s", 1, 0, 512),
+                    ("s", 1, 0, 256),
+                    ("g", 1, 256, 384),
+                    ("g", 1, 384, 512),
                     ("g", 2, 0, 128),
                     ("g", 2, 128, 256),
                     ("g", 2, 256, 384),
@@ -230,7 +250,7 @@ def tile_ryeelman_pa_t_kernel(
         def inv_transposes(m):
             inv_ps[m] = ps_n.tile([P, 512], F32, name="n_t")
             for tt in range(2):
-                words = inv_all[:, 2 * m + tt, :].bitcast(F32)
+                words = inv_all[:, row(2 * m + tt), :].bitcast(F32)
                 for u in range(2):
                     nc.tensor.transpose(
                         out=inv_ps[m][:, P * (2 * u + tt) : P * (2 * u + tt) + P],
@@ -260,80 +280,91 @@ def tile_ryeelman_pa_t_kernel(
                     for w in range(2):
                         wc = slice(256 * g + P * w, 256 * g + P * w + P)
                         nc.tensor.matmul_mx(
-                            out=acc[t, w][:, P * j : P * j + P],
-                            lhsT=codes[t][:, rows].bitcast(FP8X4),
-                            lhsT_scale=scl[t][:, rows],
-                            rhs=wcodes[:, wc].bitcast(FP8X4),
-                            rhs_scale=wscl[:, wc],
+                            out=acc[t, w][:, P * (j + w) : P * (j + w) + P],
+                            lhsT=wcodes[:, wc].bitcast(FP8X4),
+                            lhsT_scale=wscl[:, wc],
+                            rhs=codes[t][:, rows].bitcast(FP8X4),
+                            rhs_scale=scl[t][:, rows],
                             start=(g == 0),
                             stop=(g == 1),
                         )
             rows = slice(P * t, P * t + P)
             nc.tensor.matmul_mx(
-                out=acc[t, 1][:, 3 * P : 4 * P],
-                lhsT=icodes[:, rows].bitcast(FP8X4),
-                lhsT_scale=iscl[:, rows],
-                rhs=wicodes[:].bitcast(FP8X4),
-                rhs_scale=wiscl[:],
+                out=acc[t, 1][:, 0:P],
+                lhsT=wicodes[:].bitcast(FP8X4),
+                lhsT_scale=wiscl[:],
+                rhs=icodes[:, rows].bitcast(FP8X4),
+                rhs_scale=iscl[:, rows],
                 start=True,
                 stop=True,
             )
 
+        def add_up(t):
+            if t == NT - 1:
+                acc[NT, 0] = ps_o.tile([P, 512], F32, name="acc_l")
+            base = H * (NT - t)
+            terms = [prod[:, base + H * j : base + H * j + H] for j in range(NJ)]
+            terms = [bias_t[:], rr[:, t % 3, 0:H]] + terms
+            for i, term in enumerate(terms):
+                nc.tensor.matmul(
+                    out=acc[t + 1, 0][:, 3 * H : 4 * H],
+                    lhsT=term,
+                    rhs=ident[:],
+                    is_transpose=True,
+                    start=(i == 0),
+                    stop=(i == len(terms) - 1),
+                )
+
         def right_out(t):
-            if t % 2 == 0:
-                rs[t // 2] = work.tile([P, 2, 512], F32, name="rs")
-            nc.scalar.copy(out=rs[t // 2][:, t % 2, :], in_=acc[t, 1][:])
+            nc.scalar.copy(out=rr[:, t % 3, 0 : 4 * H], in_=acc[t, 1][:])
 
         def left_times_right(t):
+            n = 4 * H if t > 0 else 3 * H
+            base = H * (NT - t)
             nc.vector.tensor_tensor(
-                out=rs[t // 2][:, t % 2, 0:384],
-                in0=acc[t, 0][:, 0:384],
-                in1=rs[t // 2][:, t % 2, 0:384],
+                out=prod[:, base : base + n],
+                in0=acc[t, 0][:, 0:n],
+                in1=rr[:, t % 3, H : H + n],
                 op=ALU.mult,
             )
 
-        def add_up(m, eng):
-            half = work.tile([P, 2, 256], F32, name="half")
-            eng.tensor_tensor(
-                out=half[:], in0=rs[m][:, :, 0:256], in1=rs[m][:, :, 256:512], op=ALU.add
-            )
-            quarter = work.tile([P, 2, H], F32, name="quarter")
-            eng.tensor_tensor(
-                out=quarter[:], in0=half[:, :, 0:H], in1=half[:, :, H : 2 * H], op=ALU.add
-            )
-            eng.tensor_tensor(
-                out=pre_all[:, 2 * m : 2 * m + 2, :],
-                in0=quarter[:],
-                in1=bias_bf[:].unsqueeze(1).to_broadcast([P, 2, H]),
-                op=ALU.add,
-            )
-
         def finish(t0, t1):
-            nc.scalar.activation(out=pre_all[:, t0:t1, :], in_=pre_all[:, t0:t1, :], func=ACT.Tanh)
-            nc.sync.dma_start(out=out_v[:, t0:t1, :], in_=pre_all[:, t0:t1, :])
+            q0, q1 = row(t1 - 1), row(t0) + 1
+            c0, c1 = 3 * H + H * q0, 3 * H + H * q1
+            if t1 == NT:
+                nc.scalar.activation(out=prod[:, c0 : c0 + H], in_=acc[NT, 0][:, 3 * H : 4 * H], func=ACT.Tanh)
+                c2 = c0 + H
+            else:
+                c2 = c0
+            nc.scalar.activation(out=prod[:, c2:c1], in_=prod[:, c2:c1], func=ACT.Tanh)
+            nc.sync.dma_start(
+                out=out_v[:, q0:q1, :], in_=prod[:, c0:c1].rearrange("p (t h) -> p t h", h=H)
+            )
 
         def has(t):
             return 0 <= t < NT
 
         for k in range(-5, NT + 1):
-            m = (k + 1) // 2
-            inv_now = k % 2 == 1 and 0 <= m < NT // 2
+            m = k // 2
+            inv_now = k % 2 == 0 and 0 <= m < NT // 2
             if has(k + 1):
                 reciprocal(k + 1)
             if has(k - 1):
                 products(k - 1)
+            if has(k - 2):
+                add_up(k - 2)
+            if has(k - 1):
                 right_out(k - 1)
-            if k == NT - 1:
+            if k == NT - 2:
                 finish(0, 16)
+            if k == NT - 1:
                 finish(16, 28)
-            if k == NT:
-                finish(28, 30)
             if inv_now:
                 inv_transposes(m)
             if k == -1:
                 raw_transposes(0)
-            if k == -1:
                 prepare_weights()
+                prepare_bias()
             if inv_now:
                 inv_copy(m)
             if has(k):
@@ -347,19 +378,26 @@ def tile_ryeelman_pa_t_kernel(
             if inv_now:
                 inv_quantise(m)
             if k == 0:
-                nc.vector.tensor_copy(out=blk0[:, NJ * 4 :, 1:16], in_=hid15[:, NJ * 4 :, 0:15])
+                place_first_channels(NT - 12, NT - 4)
+            if k == 7:
+                place_first_channels(0, NT - 12)
             if has(k + 2):
                 norm_transposes(k + 2)
             if has(k + 1) and k != -1:
                 raw_transposes(k + 1)
             if has(k + 5):
                 load(k + 5)
-            if -4 <= k <= -1:
-                load_inv(k + 4)
+            if k == -4:
+                load_weights()
+            if -3 <= k <= 0:
+                load_inv(k + 3)
+            if k == -3:
+                load_first_channels(NT - 12, NT - 4)
+            if k == 2:
+                load_first_channels(0, NT - 12)
             if has(k + 3):
                 squares(k + 3)
             if has(k + 4):
                 first_channels(k + 4)
-            if has(k - 1) and (k - 1) % 2 == 1:
-                add_up((k - 1) // 2, nc.vector if k == NT else nc.gpsimd)
-        finish(30, 32)
+        add_up(NT - 1)
+        finish(28, NT)

@@ -103,6 +103,7 @@ def tile_ryeelman_pa_t_kernel(
         rr = const.tile([P, 3, 5 * H], F32, name="rr")
         for i in range(3):
             nc.vector.memset(rr[:, i, 4 * H : 5 * H], 1.0)
+        turn = const.tile([P, 1], U32, name="turn")
         bias_f = const.tile([P, H], F32, name="bias_f")
         bias_t = const.tile([P, P], F32, name="bias_t")
 
@@ -170,13 +171,11 @@ def tile_ryeelman_pa_t_kernel(
                 plan = (
                     ("s", 0, 0, 512),
                     ("s", 1, 0, 256),
-                    ("g", 1, 256, 384),
-                    ("g", 1, 384, 512),
-                    ("g", 2, 0, 128),
-                    ("g", 2, 128, 256),
-                    ("g", 2, 256, 384),
-                    ("g", 2, 384, 512),
+                    ("g", 2, 0, 512),
+                    ("g", 1, 256, 512),
                 )
+            if t >= 4:
+                nc.gpsimd.tensor_copy(out=turn[:], in_=codes[t - 4][:, 767:768])
             for who, j, q0, q1 in plan:
                 src = big[t][:, j, 2 * q0 : 2 * q1].rearrange("p (q e) -> p e q", e=2)
                 dst = sq[t][:, j, :, q0:q1]

@@ -17,6 +17,7 @@ NJ = 3
 CC = 1024
 H = 128
 EPS = 1e-6
+SPLIT = 128
 FLOPS = 2 * 4096 * 3 * 1024 * 256 + 2 * 4096 * 512 * 128
 
 
@@ -165,26 +166,28 @@ def tile_ryeelman_pa_t_kernel(
 
         def squares(t):
             sq[t] = work.tile([P, NJ, 2, 512], F32, name="sq")
-            if t < 2:
-                plan = (("s", 0, 0, 512), ("v", 1, 0, 512), ("s", 2, 0, 256), ("v", 2, 256, 512))
-            else:
-                plan = (
-                    ("s", 0, 0, 512),
-                    ("s", 1, 0, 256),
-                    ("g", 2, 0, 512),
-                    ("g", 1, 256, 512),
-                )
             if t >= 4:
                 nc.gpsimd.tensor_copy(out=turn[:], in_=codes[t - 4][:, 767:768])
-            for who, j, q0, q1 in plan:
-                src = big[t][:, j, 2 * q0 : 2 * q1].rearrange("p (q e) -> p e q", e=2)
-                dst = sq[t][:, j, :, q0:q1]
-                if who == "s":
+            if t < 2:
+                plan = (
+                    (nc.scalar, 0, 1, 0, 512),
+                    (nc.vector, 1, 2, 0, 512),
+                    (nc.scalar, 2, 3, 0, 256),
+                    (nc.vector, 2, 3, 256, 512),
+                )
+            else:
+                plan = (
+                    (nc.scalar, 0, 1, 0, 512),
+                    (nc.scalar, 1, 3, 0, SPLIT),
+                    (nc.gpsimd, 1, 3, SPLIT, 512),
+                )
+            for eng, j0, j1, q0, q1 in plan:
+                src = big[t][:, j0:j1, 2 * q0 : 2 * q1].rearrange("p j (q e) -> p j e q", e=2)
+                dst = sq[t][:, j0:j1, :, q0:q1]
+                if eng is nc.scalar:
                     nc.scalar.activation(out=dst, in_=src, func=ACT.Square)
-                elif who == "v":
-                    nc.vector.tensor_tensor(out=dst, in0=src, in1=src, op=ALU.mult)
                 else:
-                    nc.gpsimd.tensor_tensor(out=dst, in0=src, in1=src, op=ALU.mult)
+                    eng.tensor_tensor(out=dst, in0=src, in1=src, op=ALU.mult)
 
         def norm_transposes(t):
             for g in (1, 0):

@@ -153,7 +153,8 @@ def tile_ryeelman_pa_t_kernel(
 
         def load(t):
             big[t] = bigp.tile([P, NJ, CC], BF16, name="big")
-            nc.sync.dma_start(out=big[t][:, :, 16:CC], in_=hid[:, row(t), :, 15 : CC - 1])
+            for c0, c1 in ((512, CC), (16, 512)) if t == 0 else ((16, CC),):
+                nc.sync.dma_start(out=big[t][:, :, c0:c1], in_=hid[:, row(t), :, c0 - 1 : c1 - 1])
 
         def first_channels(t):
             q = row(t)
@@ -168,7 +169,18 @@ def tile_ryeelman_pa_t_kernel(
             sq[t] = work.tile([P, NJ, 2, 512], F32, name="sq")
             if t >= 4:
                 nc.gpsimd.tensor_copy(out=turn[:], in_=codes[t - 4][:, 767:768])
-            if t < 2:
+            if t == 0:
+                plan = (
+                    (nc.scalar, 0, 1, 256, 512),
+                    (nc.vector, 1, 2, 256, 512),
+                    (nc.scalar, 2, 3, 256, 384),
+                    (nc.vector, 2, 3, 384, 512),
+                    (nc.scalar, 0, 1, 0, 256),
+                    (nc.vector, 1, 2, 0, 256),
+                    (nc.scalar, 2, 3, 0, 128),
+                    (nc.vector, 2, 3, 128, 256),
+                )
+            elif t < 2:
                 plan = (
                     (nc.scalar, 0, 1, 0, 512),
                     (nc.vector, 1, 2, 0, 512),
@@ -214,7 +226,8 @@ def tile_ryeelman_pa_t_kernel(
                     bias=eps_t[:, 0:1],
                 )
             recip[t] = work.tile([P, CC], F32, name="recip")
-            nc.scalar.activation(out=recip[t][:], in_=n2[:], func=ACT.Square)
+            for c0, c1 in ((512, CC), (0, 512)) if t == 0 else ((0, CC),):
+                nc.scalar.activation(out=recip[t][:, c0:c1], in_=n2[:, c0:c1], func=ACT.Square)
 
         def raw_transposes(t):
             words = big[t][:].bitcast(F32)
@@ -228,21 +241,22 @@ def tile_ryeelman_pa_t_kernel(
                             identity=ident[:],
                         )
 
-        def scale(t, j):
-            if j == 0:
+        def scale(t, j, x0=0, x1=256):
+            if t not in grp:
                 grp[t] = work.tile([P, NJ, CC], BF16, name="grp", align_bytes=64)
             nc.vector.tensor_tensor(
-                out=grp[t][:, j, :].rearrange("p (x u e) -> p x u e", u=2, e=2),
-                in0=eq_t[t, j][:].bitcast(BF16).rearrange("p (u x e) -> p x u e", u=2, e=2),
-                in1=recip[t][:].rearrange("p (x u e) -> p x u e", u=2, e=2),
+                out=grp[t][:, j, :].rearrange("p (x u e) -> p x u e", u=2, e=2)[:, x0:x1],
+                in0=eq_t[t, j][:].bitcast(BF16).rearrange("p (u x e) -> p x u e", u=2, e=2)[:, x0:x1],
+                in1=recip[t][:].rearrange("p (x u e) -> p x u e", u=2, e=2)[:, x0:x1],
                 op=ALU.mult,
             )
 
-        def quantise(t):
-            codes[t] = work.tile([P, NJ * 256], U32, name="codes", align_bytes=64)
-            scl[t] = work.tile([P, NJ * 256], U8, name="scl", align_bytes=64)
+        def quantise(t, pieces=((0, 512), (512, 768))):
+            if t not in codes:
+                codes[t] = work.tile([P, NJ * 256], U32, name="codes", align_bytes=64)
+                scl[t] = work.tile([P, NJ * 256], U8, name="scl", align_bytes=64)
             flat = grp[t][:].rearrange("p j c -> p (j c)")
-            for w0, w1 in ((0, 512), (512, 768)):
+            for w0, w1 in pieces:
                 nc.vector.quantize_mx(
                     out=codes[t][:, w0:w1].bitcast(FP8X4),
                     scales=scl[t][:, w0:w1],
@@ -273,23 +287,22 @@ def tile_ryeelman_pa_t_kernel(
                 out=icodes[:, cols].bitcast(FP8X4), scales=iscl[:, cols], in_=inv_g[m][:]
             )
 
-        def products(t):
-            acc[t, 0] = ps_o.tile([P, 512], F32, name="acc_l")
-            acc[t, 1] = ps_o.tile([P, 512], F32, name="acc_r")
-            for j in range(NJ):
-                for g in range(2):
-                    rows = slice(256 * j + P * g, 256 * j + P * g + P)
-                    for w in range(2):
-                        wc = slice(256 * g + P * w, 256 * g + P * w + P)
-                        nc.tensor.matmul_mx(
-                            out=acc[t, w][:, P * (j + w) : P * (j + w) + P],
-                            lhsT=wcodes[:, wc].bitcast(FP8X4),
-                            lhsT_scale=wscl[:, wc],
-                            rhs=codes[t][:, rows].bitcast(FP8X4),
-                            rhs_scale=scl[t][:, rows],
-                            start=(g == 0),
-                            stop=(g == 1),
-                        )
+        def left_right(t, j, left, right):
+            for g in range(2):
+                rows = slice(256 * j + P * g, 256 * j + P * g + P)
+                for w, dst in ((0, left), (1, right)):
+                    wc = slice(256 * g + P * w, 256 * g + P * w + P)
+                    nc.tensor.matmul_mx(
+                        out=dst,
+                        lhsT=wcodes[:, wc].bitcast(FP8X4),
+                        lhsT_scale=wscl[:, wc],
+                        rhs=codes[t][:, rows].bitcast(FP8X4),
+                        rhs_scale=scl[t][:, rows],
+                        start=(g == 0),
+                        stop=(g == 1),
+                    )
+
+        def lin(t):
             rows = slice(P * t, P * t + P)
             nc.tensor.matmul_mx(
                 out=acc[t, 1][:, 0:P],
@@ -301,21 +314,27 @@ def tile_ryeelman_pa_t_kernel(
                 stop=True,
             )
 
-        def add_up(t):
-            if t == NT - 1:
-                acc[NT, 0] = ps_o.tile([P, 512], F32, name="acc_l")
-            base = H * (NT - t)
-            terms = [prod[:, base + H * j : base + H * j + H] for j in range(NJ)]
-            terms = [bias_t[:], rr[:, t % 3, 0:H]] + terms
+        def products(t):
+            acc[t, 0] = ps_o.tile([P, 512], F32, name="acc_l")
+            acc[t, 1] = ps_o.tile([P, 512], F32, name="acc_r")
+            for j in range(NJ):
+                left_right(t, j, acc[t, 0][:, P * j : P * j + P], acc[t, 1][:, P * (j + 1) : P * (j + 2)])
+            lin(t)
+
+        def add_up(t, dst, terms):
             for i, term in enumerate(terms):
                 nc.tensor.matmul(
-                    out=acc[t + 1, 0][:, 3 * H : 4 * H],
+                    out=dst,
                     lhsT=term,
                     rhs=ident[:],
                     is_transpose=True,
                     start=(i == 0),
                     stop=(i == len(terms) - 1),
                 )
+
+        def terms_of(t):
+            base = H * (NT - t)
+            return [bias_t[:], rr[:, t % 3, 0:H]] + [prod[:, base + H * j : base + H * j + H] for j in range(NJ)]
 
         def right_out(t):
             nc.scalar.copy(out=rr[:, t % 3, 0 : 4 * H], in_=acc[t, 1][:])
@@ -333,12 +352,7 @@ def tile_ryeelman_pa_t_kernel(
         def finish(t0, t1):
             q0, q1 = row(t1 - 1), row(t0) + 1
             c0, c1 = 3 * H + H * q0, 3 * H + H * q1
-            if t1 == NT:
-                nc.scalar.activation(out=prod[:, c0 : c0 + H], in_=acc[NT, 0][:, 3 * H : 4 * H], func=ACT.Tanh)
-                c2 = c0 + H
-            else:
-                c2 = c0
-            nc.scalar.activation(out=prod[:, c2:c1], in_=prod[:, c2:c1], func=ACT.Tanh)
+            nc.scalar.activation(out=prod[:, c0:c1], in_=prod[:, c0:c1], func=ACT.Tanh)
             nc.sync.dma_start(
                 out=out_v[:, q0:q1, :], in_=prod[:, c0:c1].rearrange("p (t h) -> p t h", h=H)
             )
@@ -346,7 +360,7 @@ def tile_ryeelman_pa_t_kernel(
         def has(t):
             return 0 <= t < NT
 
-        for k in range(-5, NT + 1):
+        for k in range(-5, NT):
             m = k // 2
             inv_now = k % 2 == 0 and 0 <= m < NT // 2
             if has(k + 1):
@@ -354,7 +368,7 @@ def tile_ryeelman_pa_t_kernel(
             if has(k - 1):
                 products(k - 1)
             if has(k - 2):
-                add_up(k - 2)
+                add_up(k - 2, acc[k - 1, 0][:, 3 * H : 4 * H], terms_of(k - 2))
             if has(k - 1):
                 right_out(k - 1)
             if k == NT - 2:
@@ -369,13 +383,23 @@ def tile_ryeelman_pa_t_kernel(
                 prepare_bias()
             if inv_now:
                 inv_copy(m)
-            if has(k):
+            if k == NT - 1:
                 scale(k, 0)
                 scale(k, 1)
-                scale(k, 2)
-            if has(k - 1):
                 left_times_right(k - 1)
-            if has(k):
+                quantise(k, ((0, 256),))
+                scale(k, 2)
+                quantise(k, ((256, 512), (512, 768)))
+            elif k == 0:
+                for x0 in (128, 0):
+                    for j in range(NJ):
+                        scale(k, j, x0, x0 + 128)
+            elif has(k):
+                for j in range(NJ):
+                    scale(k, j)
+            if has(k - 1) and k < NT - 1:
+                left_times_right(k - 1)
+            if has(k) and k < NT - 1:
                 quantise(k)
             if inv_now:
                 inv_quantise(m)
@@ -401,5 +425,31 @@ def tile_ryeelman_pa_t_kernel(
                 squares(k + 3)
             if has(k + 4):
                 first_channels(k + 4)
-        add_up(NT - 1)
-        finish(28, NT)
+
+        t = NT - 1
+        slot = t % 3
+        acc[t, 0] = ps_n.tile([P, 512], F32, name="n_t")
+        acc[t, 1] = ps_n.tile([P, 512], F32, name="n_t")
+        left_2 = ps_n.tile([P, 512], F32, name="n_t")
+        right_2 = ps_e.tile([P, 512], F32, name="eq_t")
+        sums = ps_o.tile([P, 512], F32, name="acc_l")
+        for j in range(2):
+            left_right(t, j, acc[t, 0][:, P * j : P * j + P], acc[t, 1][:, P * (j + 1) : P * (j + 2)])
+            if j == 0:
+                lin(t)
+                add_up(t - 1, sums[:, H : 2 * H], terms_of(t - 1))
+        left_right(t, 2, left_2[:, 0:P], right_2[:, 0:P])
+        nc.scalar.copy(out=rr[:, slot, 0 : 3 * H], in_=acc[t, 1][:, 0 : 3 * H])
+        nc.scalar.activation(out=prod[:, 5 * H : 7 * H], in_=prod[:, 5 * H : 7 * H], func=ACT.Tanh)
+        nc.vector.tensor_tensor(
+            out=prod[:, H : 3 * H], in0=acc[t, 0][:, 0 : 2 * H], in1=rr[:, slot, H : 3 * H], op=ALU.mult
+        )
+        nc.scalar.copy(out=rr[:, slot, 3 * H : 4 * H], in_=right_2[:, 0:P])
+        nc.vector.tensor_tensor(
+            out=prod[:, 0:H], in0=left_2[:, 0:P], in1=rr[:, slot, 3 * H : 4 * H], op=ALU.mult
+        )
+        add_up(t, sums[:, 0:H], [bias_t[:], rr[:, slot, 0:H], prod[:, H : 2 * H], prod[:, 2 * H : 3 * H], prod[:, 0:H]])
+        nc.scalar.activation(out=prod[:, 3 * H : 5 * H], in_=sums[:, 0 : 2 * H], func=ACT.Tanh)
+        nc.sync.dma_start(
+            out=out_v[:, 0:4, :], in_=prod[:, 3 * H : 7 * H].rearrange("p (t h) -> p t h", h=H)
+        )

@@ -17,7 +17,7 @@ NJ = 3
 CC = 1024
 H = 128
 EPS = 1e-6
-SPLIT = 128
+SPLIT = 256
 FLOPS = 2 * 4096 * 3 * 1024 * 256 + 2 * 4096 * 512 * 128
 
 
@@ -180,18 +180,10 @@ def tile_ryeelman_pa_t_kernel(
                     (nc.scalar, 2, 3, 0, 128),
                     (nc.vector, 2, 3, 128, 256),
                 )
-            elif t < 2:
-                plan = (
-                    (nc.scalar, 0, 1, 0, 512),
-                    (nc.vector, 1, 2, 0, 512),
-                    (nc.scalar, 2, 3, 0, 256),
-                    (nc.vector, 2, 3, 256, 512),
-                )
             else:
                 plan = (
-                    (nc.scalar, 0, 1, 0, 512),
-                    (nc.scalar, 1, 3, 0, SPLIT),
-                    (nc.gpsimd, 1, 3, SPLIT, 512),
+                    (nc.scalar, 0, 3, 0, SPLIT),
+                    (nc.vector if t == 1 else nc.gpsimd, 0, 3, SPLIT, 512),
                 )
             for eng, j0, j1, q0, q1 in plan:
                 src = big[t][:, j0:j1, 2 * q0 : 2 * q1].rearrange("p j (q e) -> p j e q", e=2)
@@ -371,10 +363,8 @@ def tile_ryeelman_pa_t_kernel(
                 add_up(k - 2, acc[k - 1, 0][:, 3 * H : 4 * H], terms_of(k - 2))
             if has(k - 1):
                 right_out(k - 1)
-            if k == NT - 2:
-                finish(0, 16)
             if k == NT - 1:
-                finish(16, 28)
+                finish(8, 28)
             if inv_now:
                 inv_transposes(m)
             if k == -1:
@@ -383,6 +373,8 @@ def tile_ryeelman_pa_t_kernel(
                 prepare_bias()
             if inv_now:
                 inv_copy(m)
+            if k == NT - 2:
+                finish(0, 8)
             if k == NT - 1:
                 scale(k, 0)
                 scale(k, 1)

@@ -46,7 +46,7 @@ def tile_ryeelman_pa_t_kernel(
     with ExitStack() as ctx:
         ctx.enter_context(tc.manual_schedule())
         const = ctx.enter_context(tc.tile_pool(name="const", bufs=1))
-        bigp = ctx.enter_context(tc.tile_pool(name="bigp", bufs=5))
+        bigp = ctx.enter_context(tc.tile_pool(name="bigp", bufs=3))
         work = ctx.enter_context(tc.tile_pool(name="work", bufs=2))
         ps_n = ctx.enter_context(tc.psum_pool(name="ps_n", bufs=3))
         ps_e = ctx.enter_context(tc.psum_pool(name="ps_e", bufs=3))
@@ -61,6 +61,20 @@ def tile_ryeelman_pa_t_kernel(
         ident = const.tile([P, P], F32, name="ident")
         make_identity(nc, ident[:])
 
+        pair = {}
+        big = {}
+
+        def load_columns(t, c0, c1):
+            if t // 2 not in pair:
+                pair[t // 2] = bigp.tile([P, 2, NJ, CC], BF16, name="big")
+            big[t] = pair[t // 2][:, 1 - t % 2]
+            if t > 0:
+                nc.sync.dma_start(out=big[t][:, :, c0:c1], in_=hid[:, row(t), :, c0 - 1 : c1 - 1])
+            else:
+                for j in range(NJ):
+                    nc.sync.dma_start(out=big[t][:, j, c0:c1], in_=hid[:, row(t), j, c0 - 1 : c1 - 1])
+
+        load_columns(0, 512, CC)
         inp = const.tile([P, NT * NJ], BF16, name="inp")
         nc.sync.dma_start(out=inp[:], in_=equivariant_input.rearrange("(p t) j -> p (t j)", t=NT))
         hid15 = const.tile([P, NT * NJ, 16], BF16, name="hid15")
@@ -72,6 +86,7 @@ def tile_ryeelman_pa_t_kernel(
             )
 
         load_first_channels(NT - 4, NT)
+        load_columns(0, 16, 512)
         wraw = const.tile([P, 2, 2, 4, H], BF16, name="wraw")
         wiraw = const.tile([P, 4, H], BF16, name="wiraw")
         bias_bf = const.tile([P, H], BF16, name="bias_bf")
@@ -89,13 +104,11 @@ def tile_ryeelman_pa_t_kernel(
             nc.sync.dma_start(out=bias_bf[:], in_=b_ii.partition_broadcast(P))
 
         blk0 = const.tile([P, NT * NJ, 16], BF16, name="blk0")
-        nc.vector.tensor_copy(out=blk0[:, :, 0:1], in_=inp[:].unsqueeze(2))
 
         def place_first_channels(q0, q1):
             rows = slice(NJ * q0, NJ * q1)
             nc.vector.tensor_copy(out=blk0[:, rows, 1:16], in_=hid15[:, rows, 0:15])
 
-        place_first_channels(NT - 4, NT)
 
         inv_all = const.tile([P, NT, 512], BF16, name="inv_all")
         icodes = const.tile([P, NT * P], U32, name="icodes", align_bytes=64)
@@ -115,13 +128,15 @@ def tile_ryeelman_pa_t_kernel(
         wicodes = const.tile([P, H], U32, name="wicodes", align_bytes=64)
         wiscl = const.tile([P, H], U8, name="wiscl", align_bytes=64)
 
-        def prepare_weights():
+        def group_weights():
             for g in range(2):
                 nc.vector.tensor_copy(
                     out=wgrp[:, g].rearrange("p (w h) t -> p w h t", w=2),
                     in_=wraw[:, :, g].rearrange("p w t h -> p w h t"),
                 )
             nc.vector.tensor_copy(out=wigrp[:], in_=wiraw[:].rearrange("p t h -> p h t"))
+
+        def quantise_weights():
             nc.vector.quantize_mx(
                 out=wcodes[:].bitcast(FP8X4),
                 scales=wscl[:],
@@ -133,13 +148,14 @@ def tile_ryeelman_pa_t_kernel(
                 in_=wigrp[:].rearrange("p h t -> p (h t)"),
             )
 
-        def prepare_bias():
+        def transpose_bias():
             nc.vector.tensor_copy(out=bias_f[:], in_=bias_bf[:])
-            ps = ps_o.tile([P, 512], F32, name="acc_l")
-            nc.tensor.transpose(out=ps[:, 0:P], in_=bias_f[:], identity=ident[:])
-            nc.vector.tensor_copy(out=bias_t[:], in_=ps[:, 0:P])
+            acc[-1, 0] = ps_o.tile([P, 512], F32, name="acc_l")
+            nc.tensor.transpose(out=acc[-1, 0][:, 0:P], in_=bias_f[:], identity=ident[:])
 
-        big = {}
+        def keep_bias():
+            nc.vector.tensor_copy(out=bias_t[:], in_=acc[-1, 0][:, 0:P])
+
         sq = {}
         n_t = {}
         recip = {}
@@ -152,38 +168,29 @@ def tile_ryeelman_pa_t_kernel(
         inv_g = {}
 
         def load(t):
-            big[t] = bigp.tile([P, NJ, CC], BF16, name="big")
-            for c0, c1 in ((512, CC), (16, 512)) if t == 0 else ((16, CC),):
-                nc.sync.dma_start(out=big[t][:, :, c0:c1], in_=hid[:, row(t), :, c0 - 1 : c1 - 1])
+            load_columns(t, 16, CC)
 
-        def first_channels(t):
-            q = row(t)
-            nc.scalar.copy(out=big[t][:, :, 0:16], in_=blk0[:, NJ * q : NJ * q + NJ, :])
+        def first_channels(i):
+            q = row(2 * i + 1)
+            nc.scalar.copy(
+                out=pair[i][:, :, :, 0:16],
+                in_=blk0[:, NJ * q : NJ * q + 2 * NJ, :].rearrange("p (t j) c -> p t j c", j=NJ),
+            )
 
-        def load_inv(c):
-            ts = slice(NT - 8 * c - 8, NT - 8 * c)
+        def load_inv(t0, t1):
+            ts = slice(row(t1 - 1), row(t0) + 1)
             nc.sync.dma_start(out=inv_all[:, ts, 0:384], in_=ii_v[:, ts, :])
             nc.sync.dma_start(out=inv_all[:, ts, 384:512], in_=ih_v[:, ts, :])
 
-        def squares(t):
-            sq[t] = work.tile([P, NJ, 2, 512], F32, name="sq")
+        def squares(t, plan=None):
+            if t not in sq:
+                sq[t] = work.tile([P, NJ, 2, 512], F32, name="sq")
             if t >= 4:
                 nc.gpsimd.tensor_copy(out=turn[:], in_=codes[t - 4][:, 767:768])
-            if t == 0:
-                plan = (
-                    (nc.scalar, 0, 1, 256, 512),
-                    (nc.vector, 1, 2, 256, 512),
-                    (nc.scalar, 2, 3, 256, 384),
-                    (nc.vector, 2, 3, 384, 512),
-                    (nc.scalar, 0, 1, 0, 256),
-                    (nc.vector, 1, 2, 0, 256),
-                    (nc.scalar, 2, 3, 0, 128),
-                    (nc.vector, 2, 3, 128, 256),
-                )
-            else:
+            if plan is None:
                 plan = (
                     (nc.scalar, 0, 3, 0, SPLIT),
-                    (nc.vector if t == 1 else nc.gpsimd, 0, 3, SPLIT, 512),
+                    (nc.vector if t < 3 else nc.gpsimd, 0, 3, SPLIT, 512),
                 )
             for eng, j0, j1, q0, q1 in plan:
                 src = big[t][:, j0:j1, 2 * q0 : 2 * q1].rearrange("p j (q e) -> p j e q", e=2)
@@ -352,7 +359,21 @@ def tile_ryeelman_pa_t_kernel(
         def has(t):
             return 0 <= t < NT
 
-        for k in range(-5, NT):
+        for q0 in (256, 0):
+            if q0 == 0:
+                nc.vector.tensor_copy(out=blk0[:, :, 0:1], in_=inp[:].unsqueeze(2))
+                place_first_channels(NT - 4, NT)
+                first_channels(0)
+            plan = (
+                (nc.scalar, 0, 1, q0, q0 + 256),
+                (nc.vector, 1, 2, q0, q0 + 256),
+                (nc.scalar, 2, 3, q0, q0 + 128),
+                (nc.vector, 2, 3, q0 + 128, q0 + 256),
+            )
+            squares(0, plan)
+
+        inv_loads = {-2: (0, 4), 0: (4, 8), 2: (8, 16), 5: (16, 24), 8: (24, 32)}
+        for k in range(-4, NT):
             m = k // 2
             inv_now = k % 2 == 0 and 0 <= m < NT // 2
             if has(k + 1):
@@ -369,8 +390,9 @@ def tile_ryeelman_pa_t_kernel(
                 inv_transposes(m)
             if k == -1:
                 raw_transposes(0)
-                prepare_weights()
-                prepare_bias()
+                transpose_bias()
+                group_weights()
+                squares(2)
             if inv_now:
                 inv_copy(m)
             if k == NT - 2:
@@ -393,9 +415,12 @@ def tile_ryeelman_pa_t_kernel(
                 left_times_right(k - 1)
             if has(k) and k < NT - 1:
                 quantise(k)
+            if k == 0:
+                quantise_weights()
             if inv_now:
                 inv_quantise(m)
             if k == 0:
+                keep_bias()
                 place_first_channels(NT - 12, NT - 4)
             if k == 7:
                 place_first_channels(0, NT - 12)
@@ -407,40 +432,40 @@ def tile_ryeelman_pa_t_kernel(
                 load(k + 5)
             if k == -4:
                 load_weights()
-            if -3 <= k <= 0:
-                load_inv(k + 3)
-            if k == -3:
+            if k in inv_loads:
+                load_inv(*inv_loads[k])
+            if k == -1:
                 load_first_channels(NT - 12, NT - 4)
             if k == 2:
                 load_first_channels(0, NT - 12)
-            if has(k + 3):
+            if has(k + 3) and k not in (-3, -1):
                 squares(k + 3)
-            if has(k + 4):
-                first_channels(k + 4)
+            if has(k + 4) and k % 2 == 0 and k != -4:
+                first_channels((k + 4) // 2)
 
         t = NT - 1
         slot = t % 3
         acc[t, 0] = ps_n.tile([P, 512], F32, name="n_t")
         acc[t, 1] = ps_n.tile([P, 512], F32, name="n_t")
-        left_2 = ps_n.tile([P, 512], F32, name="n_t")
-        right_2 = ps_e.tile([P, 512], F32, name="eq_t")
+        left_12 = ps_n.tile([P, 512], F32, name="n_t")
+        right_12 = ps_e.tile([P, 512], F32, name="eq_t")
         sums = ps_o.tile([P, 512], F32, name="acc_l")
-        for j in range(2):
-            left_right(t, j, acc[t, 0][:, P * j : P * j + P], acc[t, 1][:, P * (j + 1) : P * (j + 2)])
-            if j == 0:
-                lin(t)
-                add_up(t - 1, sums[:, H : 2 * H], terms_of(t - 1))
-        left_right(t, 2, left_2[:, 0:P], right_2[:, 0:P])
-        nc.scalar.copy(out=rr[:, slot, 0 : 3 * H], in_=acc[t, 1][:, 0 : 3 * H])
+        left_right(t, 0, acc[t, 0][:, 0:P], acc[t, 1][:, P : 2 * P])
+        lin(t)
+        add_up(t - 1, sums[:, H : 2 * H], terms_of(t - 1))
+        for j in (1, 2):
+            left_right(t, j, left_12[:, P * (j - 1) : P * j], right_12[:, P * (j - 1) : P * j])
+        nc.scalar.copy(out=rr[:, slot, 0 : 2 * H], in_=acc[t, 1][:, 0 : 2 * H])
         nc.scalar.activation(out=prod[:, 5 * H : 7 * H], in_=prod[:, 5 * H : 7 * H], func=ACT.Tanh)
         nc.vector.tensor_tensor(
-            out=prod[:, H : 3 * H], in0=acc[t, 0][:, 0 : 2 * H], in1=rr[:, slot, H : 3 * H], op=ALU.mult
+            out=prod[:, 0:H], in0=acc[t, 0][:, 0:H], in1=rr[:, slot, H : 2 * H], op=ALU.mult
         )
-        nc.scalar.copy(out=rr[:, slot, 3 * H : 4 * H], in_=right_2[:, 0:P])
+        nc.scalar.copy(out=rr[:, slot, 2 * H : 4 * H], in_=right_12[:, 0 : 2 * P])
         nc.vector.tensor_tensor(
-            out=prod[:, 0:H], in0=left_2[:, 0:P], in1=rr[:, slot, 3 * H : 4 * H], op=ALU.mult
+            out=prod[:, H : 3 * H], in0=left_12[:, 0 : 2 * P], in1=rr[:, slot, 2 * H : 4 * H], op=ALU.mult
         )
-        add_up(t, sums[:, 0:H], [bias_t[:], rr[:, slot, 0:H], prod[:, H : 2 * H], prod[:, 2 * H : 3 * H], prod[:, 0:H]])
+        terms = [bias_t[:], rr[:, slot, 0:H]] + [prod[:, H * j : H * j + H] for j in range(NJ)]
+        add_up(t, sums[:, 0:H], terms)
         nc.scalar.activation(out=prod[:, 3 * H : 5 * H], in_=sums[:, 0 : 2 * H], func=ACT.Tanh)
         nc.sync.dma_start(
             out=out_v[:, 0:4, :], in_=prod[:, 3 * H : 7 * H].rearrange("p (t h) -> p t h", h=H)

@@ -48,6 +48,8 @@ def tile_ryeelman_pa_t_kernel(
         const = ctx.enter_context(tc.tile_pool(name="const", bufs=1))
         bigp = ctx.enter_context(tc.tile_pool(name="bigp", bufs=3))
         work = ctx.enter_context(tc.tile_pool(name="work", bufs=2))
+        work3 = ctx.enter_context(tc.tile_pool(name="work3", bufs=3))
+        turns = ctx.enter_context(tc.tile_pool(name="turns", bufs=3))
         ps_n = ctx.enter_context(tc.psum_pool(name="ps_n", bufs=3))
         ps_e = ctx.enter_context(tc.psum_pool(name="ps_e", bufs=3))
         ps_o = ctx.enter_context(tc.psum_pool(name="ps_o", bufs=1))
@@ -79,13 +81,14 @@ def tile_ryeelman_pa_t_kernel(
         nc.sync.dma_start(out=inp[:], in_=equivariant_input.rearrange("(p t) j -> p (t j)", t=NT))
         hid15 = const.tile([P, NT * NJ, 16], BF16, name="hid15")
 
-        def load_first_channels(q0, q1):
+        def load_first_channels(t0, t1):
+            q0, q1 = NT - t1, NT - t0
             nc.sync.dma_start(
                 out=hid15[:, NJ * q0 : NJ * q1, 0:15],
                 in_=hid[:, q0:q1, :, 0:15].rearrange("p t j c -> p (t j) c"),
             )
 
-        load_first_channels(NT - 4, NT)
+        load_first_channels(0, 4)
         load_columns(0, 16, 512)
         wraw = const.tile([P, 2, 2, 4, H], BF16, name="wraw")
         wiraw = const.tile([P, 4, H], BF16, name="wiraw")
@@ -105,21 +108,20 @@ def tile_ryeelman_pa_t_kernel(
 
         blk0 = const.tile([P, NT * NJ, 16], BF16, name="blk0")
 
-        def place_first_channels(q0, q1):
-            rows = slice(NJ * q0, NJ * q1)
-            nc.vector.tensor_copy(out=blk0[:, rows, 1:16], in_=hid15[:, rows, 0:15])
-
+        def place_first_channels(eng, t0, t1):
+            rows = slice(NJ * (NT - t1), NJ * (NT - t0))
+            copy = nc.scalar.copy if eng is nc.scalar else eng.tensor_copy
+            copy(out=blk0[:, rows, 1:16], in_=hid15[:, rows, 0:15])
 
         inv_all = const.tile([P, NT, 512], BF16, name="inv_all")
         icodes = const.tile([P, NT * P], U32, name="icodes", align_bytes=64)
         iscl = const.tile([P, NT * P], U8, name="iscl", align_bytes=64)
         prod = const.tile([P, 3 * H + NT * H], F32, name="prod")
-        rr = const.tile([P, 3, 5 * H], F32, name="rr")
+        rr = const.tile([P, 3, 4 * H], F32, name="rr")
         for i in range(3):
-            nc.vector.memset(rr[:, i, 4 * H : 5 * H], 1.0)
-        turn = const.tile([P, 1], U32, name="turn")
+            nc.vector.memset(rr[:, i, 3 * H : 4 * H], 1.0)
         bias_f = const.tile([P, H], F32, name="bias_f")
-        bias_t = const.tile([P, P], F32, name="bias_t")
+        bias_t = const.tile([P, 1], F32, name="bias_t")
 
         wgrp = const.tile([P, 2, 2 * H, 4], BF16, name="wgrp", align_bytes=64)
         wcodes = const.tile([P, 2 * 2 * H], U32, name="wcodes", align_bytes=64)
@@ -154,7 +156,7 @@ def tile_ryeelman_pa_t_kernel(
             nc.tensor.transpose(out=acc[-1, 0][:, 0:P], in_=bias_f[:], identity=ident[:])
 
         def keep_bias():
-            nc.vector.tensor_copy(out=bias_t[:], in_=acc[-1, 0][:, 0:P])
+            nc.vector.tensor_copy(out=bias_t[:], in_=acc[-1, 0][:, 0:1])
 
         sq = {}
         n_t = {}
@@ -166,6 +168,7 @@ def tile_ryeelman_pa_t_kernel(
         acc = {}
         inv_ps = {}
         inv_g = {}
+        lin_b = {}
 
         def load(t):
             load_columns(t, 16, CC)
@@ -184,9 +187,10 @@ def tile_ryeelman_pa_t_kernel(
 
         def squares(t, plan=None):
             if t not in sq:
-                sq[t] = work.tile([P, NJ, 2, 512], F32, name="sq")
-            if t >= 4:
-                nc.gpsimd.tensor_copy(out=turn[:], in_=codes[t - 4][:, 767:768])
+                sq[t] = (
+                    work.tile([P, NJ, 2, SPLIT], F32, name="sq"),
+                    turns.tile([P, NJ, 2, 512 - SPLIT], F32, name="turn", align_bytes=64),
+                )
             if plan is None:
                 plan = (
                     (nc.scalar, 0, 3, 0, SPLIT),
@@ -194,7 +198,8 @@ def tile_ryeelman_pa_t_kernel(
                 )
             for eng, j0, j1, q0, q1 in plan:
                 src = big[t][:, j0:j1, 2 * q0 : 2 * q1].rearrange("p j (q e) -> p j e q", e=2)
-                dst = sq[t][:, j0:j1, :, q0:q1]
+                h, o = (0, 0) if q0 < SPLIT else (1, SPLIT)
+                dst = sq[t][h][:, j0:j1, :, q0 - o : q1 - o]
                 if eng is nc.scalar:
                     nc.scalar.activation(out=dst, in_=src, func=ACT.Square)
                 else:
@@ -208,7 +213,7 @@ def tile_ryeelman_pa_t_kernel(
                     for j in range(NJ):
                         nc.tensor.matmul(
                             out=n_t[t, g][:, P * r : P * r + P],
-                            lhsT=sq[t][:, j, e, 256 * g + P * u : 256 * g + P * u + P],
+                            lhsT=sq[t][g][:, j, e, P * u : P * u + P],
                             rhs=ident[:],
                             is_transpose=True,
                             start=(j == 0),
@@ -224,8 +229,8 @@ def tile_ryeelman_pa_t_kernel(
                     func=ACT.Abs_reciprocal_sqrt,
                     bias=eps_t[:, 0:1],
                 )
-            recip[t] = work.tile([P, CC], F32, name="recip")
-            for c0, c1 in ((512, CC), (0, 512)) if t == 0 else ((0, CC),):
+            recip[t] = work3.tile([P, CC], F32, name="recip")
+            for c0, c1 in ((512, CC), (0, 512)):
                 nc.scalar.activation(out=recip[t][:, c0:c1], in_=n2[:, c0:c1], func=ACT.Square)
 
         def raw_transposes(t):
@@ -240,21 +245,21 @@ def tile_ryeelman_pa_t_kernel(
                             identity=ident[:],
                         )
 
-        def scale(t, j, x0=0, x1=256):
+        def scale(t, j, g0=0, g1=2):
             if t not in grp:
-                grp[t] = work.tile([P, NJ, CC], BF16, name="grp", align_bytes=64)
+                grp[t] = turns.tile([P, 2, NJ, 512], BF16, name="turn", align_bytes=64)
             nc.vector.tensor_tensor(
-                out=grp[t][:, j, :].rearrange("p (x u e) -> p x u e", u=2, e=2)[:, x0:x1],
-                in0=eq_t[t, j][:].bitcast(BF16).rearrange("p (u x e) -> p x u e", u=2, e=2)[:, x0:x1],
-                in1=recip[t][:].rearrange("p (x u e) -> p x u e", u=2, e=2)[:, x0:x1],
+                out=grp[t][:, g0:g1, j, :].rearrange("p g (b u e) -> p g b u e", u=2, e=2),
+                in0=eq_t[t, j][:].bitcast(BF16).rearrange("p (u g b e) -> p g b u e", u=2, g=2, e=2)[:, g0:g1],
+                in1=recip[t][:].rearrange("p (g b u e) -> p g b u e", g=2, u=2, e=2)[:, g0:g1],
                 op=ALU.mult,
             )
 
         def quantise(t, pieces=((0, 512), (512, 768))):
             if t not in codes:
-                codes[t] = work.tile([P, NJ * 256], U32, name="codes", align_bytes=64)
-                scl[t] = work.tile([P, NJ * 256], U8, name="scl", align_bytes=64)
-            flat = grp[t][:].rearrange("p j c -> p (j c)")
+                codes[t] = work3.tile([P, NJ * 256], U32, name="codes", align_bytes=64)
+                scl[t] = work3.tile([P, NJ * 256], U8, name="scl", align_bytes=64)
+            flat = grp[t][:].rearrange("p g j c -> p (g j c)")
             for w0, w1 in pieces:
                 nc.vector.quantize_mx(
                     out=codes[t][:, w0:w1].bitcast(FP8X4),
@@ -286,9 +291,9 @@ def tile_ryeelman_pa_t_kernel(
                 out=icodes[:, cols].bitcast(FP8X4), scales=iscl[:, cols], in_=inv_g[m][:]
             )
 
-        def left_right(t, j, left, right):
+        def left_right(t, j0, j1, left, right):
             for g in range(2):
-                rows = slice(256 * j + P * g, 256 * j + P * g + P)
+                rows = slice(384 * g + P * j0, 384 * g + P * j1)
                 for w, dst in ((0, left), (1, right)):
                     wc = slice(256 * g + P * w, 256 * g + P * w + P)
                     nc.tensor.matmul_mx(
@@ -301,24 +306,29 @@ def tile_ryeelman_pa_t_kernel(
                         stop=(g == 1),
                     )
 
-        def lin(t):
-            rows = slice(P * t, P * t + P)
+        def lin(m):
+            cols = slice(2 * P * m, 2 * P * m + 2 * P)
+            inv_ps[m] = ps_n.tile([P, 512], F32, name="n_t")
             nc.tensor.matmul_mx(
-                out=acc[t, 1][:, 0:P],
+                out=inv_ps[m][:, 0 : 2 * P],
                 lhsT=wicodes[:].bitcast(FP8X4),
                 lhsT_scale=wiscl[:],
-                rhs=icodes[:, rows].bitcast(FP8X4),
-                rhs_scale=iscl[:, rows],
+                rhs=icodes[:, cols].bitcast(FP8X4),
+                rhs_scale=iscl[:, cols],
                 start=True,
                 stop=True,
             )
 
+        def lin_out(m):
+            lin_b[m] = work3.tile([P, 2 * P], F32, name="lin_b")
+            nc.scalar.activation(
+                out=lin_b[m][:], in_=inv_ps[m][:, 0 : 2 * P], func=ACT.Identity, bias=bias_t[:, 0:1]
+            )
+
         def products(t):
-            acc[t, 0] = ps_o.tile([P, 512], F32, name="acc_l")
             acc[t, 1] = ps_o.tile([P, 512], F32, name="acc_r")
-            for j in range(NJ):
-                left_right(t, j, acc[t, 0][:, P * j : P * j + P], acc[t, 1][:, P * (j + 1) : P * (j + 2)])
-            lin(t)
+            for j0, j1 in ((0, 2), (2, 3)):
+                left_right(t, j0, j1, acc[t, 0][:, P * j0 : P * j1], acc[t, 1][:, P * j0 : P * j1])
 
         def add_up(t, dst, terms):
             for i, term in enumerate(terms):
@@ -333,10 +343,12 @@ def tile_ryeelman_pa_t_kernel(
 
         def terms_of(t):
             base = H * (NT - t)
-            return [bias_t[:], rr[:, t % 3, 0:H]] + [prod[:, base + H * j : base + H * j + H] for j in range(NJ)]
+            return [lin_b[t // 2][:, P * (t % 2) : P * (t % 2) + P]] + [
+                prod[:, base + H * j : base + H * j + H] for j in range(NJ)
+            ]
 
         def right_out(t):
-            nc.scalar.copy(out=rr[:, t % 3, 0 : 4 * H], in_=acc[t, 1][:])
+            nc.scalar.copy(out=rr[:, t % 3, 0 : 3 * H], in_=acc[t, 1][:, 0 : 3 * H])
 
         def left_times_right(t):
             n = 4 * H if t > 0 else 3 * H
@@ -344,7 +356,7 @@ def tile_ryeelman_pa_t_kernel(
             nc.vector.tensor_tensor(
                 out=prod[:, base : base + n],
                 in0=acc[t, 0][:, 0:n],
-                in1=rr[:, t % 3, H : H + n],
+                in1=rr[:, t % 3, 0:n],
                 op=ALU.mult,
             )
 
@@ -362,7 +374,7 @@ def tile_ryeelman_pa_t_kernel(
         for q0 in (256, 0):
             if q0 == 0:
                 nc.vector.tensor_copy(out=blk0[:, :, 0:1], in_=inp[:].unsqueeze(2))
-                place_first_channels(NT - 4, NT)
+                place_first_channels(nc.vector, 0, 4)
                 first_channels(0)
             plan = (
                 (nc.scalar, 0, 1, q0, q0 + 256),
@@ -379,11 +391,16 @@ def tile_ryeelman_pa_t_kernel(
             if has(k + 1):
                 reciprocal(k + 1)
             if has(k - 1):
-                products(k - 1)
+                acc[k - 1, 0] = ps_o.tile([P, 512], F32, name="acc_l")
             if has(k - 2):
                 add_up(k - 2, acc[k - 1, 0][:, 3 * H : 4 * H], terms_of(k - 2))
             if has(k - 1):
+                products(k - 1)
+                if k % 2 == 1:
+                    lin(m)
                 right_out(k - 1)
+                if k % 2 == 1:
+                    lin_out(m)
             if k == NT - 1:
                 finish(8, 28)
             if inv_now:
@@ -392,6 +409,7 @@ def tile_ryeelman_pa_t_kernel(
                 raw_transposes(0)
                 transpose_bias()
                 group_weights()
+                quantise_weights()
                 squares(2)
             if inv_now:
                 inv_copy(m)
@@ -401,43 +419,46 @@ def tile_ryeelman_pa_t_kernel(
                 scale(k, 0)
                 scale(k, 1)
                 left_times_right(k - 1)
-                quantise(k, ((0, 256),))
+                quantise(k, ((0, 256), (384, 640)))
                 scale(k, 2)
-                quantise(k, ((256, 512), (512, 768)))
+                quantise(k, ((256, 384), (640, 768)))
             elif k == 0:
-                for x0 in (128, 0):
+                for g in (1, 0):
                     for j in range(NJ):
-                        scale(k, j, x0, x0 + 128)
+                        scale(k, j, g, g + 1)
             elif has(k):
                 for j in range(NJ):
                     scale(k, j)
             if has(k - 1) and k < NT - 1:
                 left_times_right(k - 1)
+            if inv_now:
+                inv_quantise(m)
+            if k == 3:
+                place_first_channels(nc.vector, 8, 16)
+            if k == 11:
+                place_first_channels(nc.vector, 16, 32)
             if has(k) and k < NT - 1:
                 quantise(k)
             if k == 0:
-                quantise_weights()
-            if inv_now:
-                inv_quantise(m)
-            if k == 0:
                 keep_bias()
-                place_first_channels(NT - 12, NT - 4)
-            if k == 7:
-                place_first_channels(0, NT - 12)
             if has(k + 2):
                 norm_transposes(k + 2)
             if has(k + 1) and k != -1:
                 raw_transposes(k + 1)
+            if k == -1:
+                load_first_channels(4, 8)
             if has(k + 5):
                 load(k + 5)
             if k == -4:
                 load_weights()
             if k in inv_loads:
                 load_inv(*inv_loads[k])
-            if k == -1:
-                load_first_channels(NT - 12, NT - 4)
-            if k == 2:
-                load_first_channels(0, NT - 12)
+            if k == 1:
+                load_first_channels(8, 16)
+            if k == 4:
+                load_first_channels(16, 32)
+            if k == 0:
+                place_first_channels(nc.scalar, 4, 8)
             if has(k + 3) and k not in (-3, -1):
                 squares(k + 3)
             if has(k + 4) and k % 2 == 0 and k != -4:
@@ -445,26 +466,24 @@ def tile_ryeelman_pa_t_kernel(
 
         t = NT - 1
         slot = t % 3
-        acc[t, 0] = ps_n.tile([P, 512], F32, name="n_t")
-        acc[t, 1] = ps_n.tile([P, 512], F32, name="n_t")
-        left_12 = ps_n.tile([P, 512], F32, name="n_t")
-        right_12 = ps_e.tile([P, 512], F32, name="eq_t")
+        left_01 = ps_n.tile([P, 512], F32, name="n_t")
+        right_01 = ps_n.tile([P, 512], F32, name="n_t")
+        left_2 = ps_e.tile([P, 512], F32, name="eq_t")
+        right_2 = ps_e.tile([P, 512], F32, name="eq_t")
         sums = ps_o.tile([P, 512], F32, name="acc_l")
-        left_right(t, 0, acc[t, 0][:, 0:P], acc[t, 1][:, P : 2 * P])
-        lin(t)
+        left_right(t, 0, 2, left_01[:, 0 : 2 * P], right_01[:, 0 : 2 * P])
         add_up(t - 1, sums[:, H : 2 * H], terms_of(t - 1))
-        for j in (1, 2):
-            left_right(t, j, left_12[:, P * (j - 1) : P * j], right_12[:, P * (j - 1) : P * j])
-        nc.scalar.copy(out=rr[:, slot, 0 : 2 * H], in_=acc[t, 1][:, 0 : 2 * H])
+        left_right(t, 2, 3, left_2[:, 0:P], right_2[:, 0:P])
+        nc.scalar.copy(out=rr[:, slot, 0 : 2 * H], in_=right_01[:, 0 : 2 * H])
         nc.scalar.activation(out=prod[:, 5 * H : 7 * H], in_=prod[:, 5 * H : 7 * H], func=ACT.Tanh)
         nc.vector.tensor_tensor(
-            out=prod[:, 0:H], in0=acc[t, 0][:, 0:H], in1=rr[:, slot, H : 2 * H], op=ALU.mult
+            out=prod[:, 0 : 2 * H], in0=left_01[:, 0 : 2 * H], in1=rr[:, slot, 0 : 2 * H], op=ALU.mult
         )
-        nc.scalar.copy(out=rr[:, slot, 2 * H : 4 * H], in_=right_12[:, 0 : 2 * P])
+        nc.scalar.copy(out=rr[:, slot, 2 * H : 3 * H], in_=right_2[:, 0:H])
         nc.vector.tensor_tensor(
-            out=prod[:, H : 3 * H], in0=left_12[:, 0 : 2 * P], in1=rr[:, slot, 2 * H : 4 * H], op=ALU.mult
+            out=prod[:, 2 * H : 3 * H], in0=left_2[:, 0:H], in1=rr[:, slot, 2 * H : 3 * H], op=ALU.mult
         )
-        terms = [bias_t[:], rr[:, slot, 0:H]] + [prod[:, H * j : H * j + H] for j in range(NJ)]
+        terms = [lin_b[t // 2][:, P : 2 * P]] + [prod[:, H * j : H * j + H] for j in range(NJ)]
         add_up(t, sums[:, 0:H], terms)
         nc.scalar.activation(out=prod[:, 3 * H : 5 * H], in_=sums[:, 0 : 2 * H], func=ACT.Tanh)
         nc.sync.dma_start(

@@ -38,7 +38,7 @@ def tile_ryeelman_pa_t_kernel(
     out,
 ):
     nc = tc.nc
-    hid = equivariant_hidden.rearrange("(p t) j c -> p t j c", t=NT)
+    hid = equivariant_hidden.rearrange("(p t) j c -> p (t j c)", t=NT)
     out_v = out.rearrange("(p t) h -> p t h", t=NT)
     ii_v = invariant_input.rearrange("(p t) k -> p t k", t=NT)
     ih_v = invariant_hidden.rearrange("(p t) k -> p t k", t=NT)
@@ -66,30 +66,23 @@ def tile_ryeelman_pa_t_kernel(
         pair = {}
         big = {}
 
-        def load_columns(t, c0, c1):
+        def new_tile(t):
             if t // 2 not in pair:
                 pair[t // 2] = bigp.tile([P, 2, NJ, CC], BF16, name="big")
             big[t] = pair[t // 2][:, 1 - t % 2]
-            if t > 0:
-                nc.sync.dma_start(out=big[t][:, :, c0:c1], in_=hid[:, row(t), :, c0 - 1 : c1 - 1])
-            else:
-                for j in range(NJ):
-                    nc.sync.dma_start(out=big[t][:, j, c0:c1], in_=hid[:, row(t), j, c0 - 1 : c1 - 1])
 
-        load_columns(0, 512, CC)
+        def load_rows(t, j, c0, c1):
+            start = (NJ * row(t) + j) * (CC - 1) - 1
+            nc.sync.dma_start(out=big[t][:, j, c0:c1], in_=hid[:, start + c0 : start + c1])
+
+        new_tile(0)
+        for j in range(NJ):
+            load_rows(0, j, 512, CC)
         inp = const.tile([P, NT * NJ], BF16, name="inp")
         nc.sync.dma_start(out=inp[:], in_=equivariant_input.rearrange("(p t) j -> p (t j)", t=NT))
-        hid15 = const.tile([P, NT * NJ, 16], BF16, name="hid15")
-
-        def load_first_channels(t0, t1):
-            q0, q1 = NT - t1, NT - t0
-            nc.sync.dma_start(
-                out=hid15[:, NJ * q0 : NJ * q1, 0:15],
-                in_=hid[:, q0:q1, :, 0:15].rearrange("p t j c -> p (t j) c"),
-            )
-
-        load_first_channels(0, 4)
-        load_columns(0, 16, 512)
+        for j in range(NJ):
+            load_rows(0, j, 0, 512)
+        last15 = const.tile([P, 16], BF16, name="last15")
         wraw = const.tile([P, 2, 2, 4, H], BF16, name="wraw")
         wiraw = const.tile([P, 4, H], BF16, name="wiraw")
         bias_bf = const.tile([P, H], BF16, name="bias_bf")
@@ -105,13 +98,6 @@ def tile_ryeelman_pa_t_kernel(
                 in_=W_ii.rearrange("(u q e) h -> q u (e h)", u=2, e=2),
             )
             nc.sync.dma_start(out=bias_bf[:], in_=b_ii.partition_broadcast(P))
-
-        blk0 = const.tile([P, NT * NJ, 16], BF16, name="blk0")
-
-        def place_first_channels(eng, t0, t1):
-            rows = slice(NJ * (NT - t1), NJ * (NT - t0))
-            copy = nc.scalar.copy if eng is nc.scalar else eng.tensor_copy
-            copy(out=blk0[:, rows, 1:16], in_=hid15[:, rows, 0:15])
 
         inv_all = const.tile([P, NT, 512], BF16, name="inv_all")
         icodes = const.tile([P, NT * P], U32, name="icodes", align_bytes=64)
@@ -170,15 +156,40 @@ def tile_ryeelman_pa_t_kernel(
         inv_g = {}
         lin_b = {}
 
-        def load(t):
-            load_columns(t, 16, CC)
-
-        def first_channels(i):
-            q = row(2 * i + 1)
-            nc.scalar.copy(
-                out=pair[i][:, :, :, 0:16],
-                in_=blk0[:, NJ * q : NJ * q + 2 * NJ, :].rearrange("p (t j) c -> p t j c", j=NJ),
+        def load_two_rows(i, s0, s1):
+            start = (NJ * row(2 * i + 1) + s0) * (CC - 1) - 1
+            n = (s1 - s0) // 2
+            nc.sync.dma_start(
+                out=pair[i][:].rearrange("p t j c -> p (t j) c")[:, s0 : min(s1, 6) : 2, :],
+                in_=hid[:, start : start + 2 * n * (CC - 1)].rearrange("p (i s) -> p i s", i=n)[:, :, 0:CC],
             )
+
+        def load(t):
+            new_tile(t)
+            s = NJ * (1 - t % 2)
+            load_two_rows(t // 2, s, s + 4)
+            load_rows(t, 1, 0, CC)
+
+        def load_pair(i):
+            new_tile(2 * i)
+            new_tile(2 * i + 1)
+            if i < NT // 2 - 1:
+                load_two_rows(i, 0, 6)
+            else:
+                nc.sync.dma_start(out=last15[:, 0:15], in_=hid[:, 0:15])
+                load_rows(2 * i + 1, 0, 16, CC)
+                load_two_rows(i, 2, 6)
+            load_two_rows(i, 1, 7)
+
+        def first_channels(t0, t1):
+            n, q = t1 - t0, row(t1 - 1)
+            s = 0 if n == 2 else 1 - t0 % 2
+            nc.scalar.copy(
+                out=pair[t0 // 2][:, s : s + n, :, 0:1],
+                in_=inp[:, NJ * q : NJ * q + n * NJ].rearrange("p (t j c) -> p t j c", j=NJ, c=1),
+            )
+            if t1 == NT:
+                nc.scalar.copy(out=big[NT - 1][:, 0, 1:16], in_=last15[:, 0:15])
 
         def load_inv(t0, t1):
             ts = slice(row(t1 - 1), row(t0) + 1)
@@ -373,9 +384,7 @@ def tile_ryeelman_pa_t_kernel(
 
         for q0 in (256, 0):
             if q0 == 0:
-                nc.vector.tensor_copy(out=blk0[:, :, 0:1], in_=inp[:].unsqueeze(2))
-                place_first_channels(nc.vector, 0, 4)
-                first_channels(0)
+                first_channels(0, 1)
             plan = (
                 (nc.scalar, 0, 1, q0, q0 + 256),
                 (nc.vector, 1, 2, q0, q0 + 256),
@@ -410,6 +419,7 @@ def tile_ryeelman_pa_t_kernel(
                 transpose_bias()
                 group_weights()
                 quantise_weights()
+                first_channels(2, 3)
                 squares(2)
             if inv_now:
                 inv_copy(m)
@@ -433,10 +443,6 @@ def tile_ryeelman_pa_t_kernel(
                 left_times_right(k - 1)
             if inv_now:
                 inv_quantise(m)
-            if k == 3:
-                place_first_channels(nc.vector, 8, 16)
-            if k == 11:
-                place_first_channels(nc.vector, 16, 32)
             if has(k) and k < NT - 1:
                 quantise(k)
             if k == 0:
@@ -445,24 +451,20 @@ def tile_ryeelman_pa_t_kernel(
                 norm_transposes(k + 2)
             if has(k + 1) and k != -1:
                 raw_transposes(k + 1)
-            if k == -1:
-                load_first_channels(4, 8)
-            if has(k + 5):
+            if k < -1 and has(k + 5):
                 load(k + 5)
+            if k >= -1 and k % 2 == 1 and has(k + 5):
+                load_pair((k + 5) // 2)
             if k == -4:
                 load_weights()
             if k in inv_loads:
                 load_inv(*inv_loads[k])
-            if k == 1:
-                load_first_channels(8, 16)
-            if k == 4:
-                load_first_channels(16, 32)
-            if k == 0:
-                place_first_channels(nc.scalar, 4, 8)
             if has(k + 3) and k not in (-3, -1):
+                if k < 1:
+                    first_channels(k + 3, k + 4)
                 squares(k + 3)
-            if has(k + 4) and k % 2 == 0 and k != -4:
-                first_channels((k + 4) // 2)
+            if has(k + 4) and k % 2 == 0 and k >= 0:
+                first_channels(k + 4, k + 6)
 
         t = NT - 1
         slot = t % 3

@@ -102,10 +102,8 @@ def tile_ryeelman_pa_t_kernel(
         inv_all = const.tile([P, NT, 512], BF16, name="inv_all")
         icodes = const.tile([P, NT * P], U32, name="icodes", align_bytes=64)
         iscl = const.tile([P, NT * P], U8, name="iscl", align_bytes=64)
-        prod = const.tile([P, 3 * H + NT * H], F32, name="prod")
-        rr = const.tile([P, 3, 4 * H], F32, name="rr")
-        for i in range(3):
-            nc.vector.memset(rr[:, i, 3 * H : 4 * H], 1.0)
+        rs = const.tile([P, 3 * H + NT * H], F32, name="rs")
+        prod = const.tile([P, 3, 3 * H], F32, name="prod")
         bias_f = const.tile([P, H], F32, name="bias_f")
         bias_t = const.tile([P, 1], F32, name="bias_t")
 
@@ -146,6 +144,7 @@ def tile_ryeelman_pa_t_kernel(
 
         sq = {}
         n_t = {}
+        n2 = {}
         recip = {}
         eq_t = {}
         grp = {}
@@ -231,18 +230,20 @@ def tile_ryeelman_pa_t_kernel(
                             stop=(j == 2),
                         )
 
-        def reciprocal(t):
-            n2 = work.tile([P, CC], F32, name="n2")
+        def root(t):
+            n2[t] = work.tile([P, CC], F32, name="n2")
             for g in (1, 0):
                 nc.scalar.activation(
-                    out=n2[:, 512 * g : 512 * g + 512].rearrange("p (b r) -> p b r", r=4),
+                    out=n2[t][:, 512 * g : 512 * g + 512].rearrange("p (b r) -> p b r", r=4),
                     in_=n_t[t, g][:].rearrange("p (r b) -> p b r", r=4),
                     func=ACT.Abs_reciprocal_sqrt,
                     bias=eps_t[:, 0:1],
                 )
+
+        def reciprocal(t):
             recip[t] = work3.tile([P, CC], F32, name="recip")
             for c0, c1 in ((512, CC), (0, 512)):
-                nc.scalar.activation(out=recip[t][:, c0:c1], in_=n2[:, c0:c1], func=ACT.Square)
+                nc.scalar.activation(out=recip[t][:, c0:c1], in_=n2[t][:, c0:c1], func=ACT.Square)
 
         def raw_transposes(t):
             words = big[t][:].bitcast(F32)
@@ -337,7 +338,7 @@ def tile_ryeelman_pa_t_kernel(
             )
 
         def products(t):
-            acc[t, 1] = ps_o.tile([P, 512], F32, name="acc_r")
+            acc[t, 0] = ps_o.tile([P, 512], F32, name="acc_l")
             for j0, j1 in ((0, 2), (2, 3)):
                 left_right(t, j0, j1, acc[t, 0][:, P * j0 : P * j1], acc[t, 1][:, P * j0 : P * j1])
 
@@ -353,30 +354,27 @@ def tile_ryeelman_pa_t_kernel(
                 )
 
         def terms_of(t):
-            base = H * (NT - t)
             return [lin_b[t // 2][:, P * (t % 2) : P * (t % 2) + P]] + [
-                prod[:, base + H * j : base + H * j + H] for j in range(NJ)
+                prod[:, t % 3, H * j : H * j + H] for j in range(NJ)
             ]
 
         def right_out(t):
-            nc.scalar.copy(out=rr[:, t % 3, 0 : 3 * H], in_=acc[t, 1][:, 0 : 3 * H])
-
-        def left_times_right(t):
             n = 4 * H if t > 0 else 3 * H
             base = H * (NT - t)
+            nc.scalar.copy(out=rs[:, base : base + n], in_=acc[t, 1][:, 0:n])
+
+        def left_times_right(t):
+            base = H * (NT - t)
             nc.vector.tensor_tensor(
-                out=prod[:, base : base + n],
-                in0=acc[t, 0][:, 0:n],
-                in1=rr[:, t % 3, 0:n],
-                op=ALU.mult,
+                out=prod[:, t % 3, :], in0=acc[t, 0][:, 0 : 3 * H], in1=rs[:, base : base + 3 * H], op=ALU.mult
             )
 
         def finish(t0, t1):
             q0, q1 = row(t1 - 1), row(t0) + 1
             c0, c1 = 3 * H + H * q0, 3 * H + H * q1
-            nc.scalar.activation(out=prod[:, c0:c1], in_=prod[:, c0:c1], func=ACT.Tanh)
+            nc.scalar.activation(out=rs[:, c0:c1], in_=rs[:, c0:c1], func=ACT.Tanh)
             nc.sync.dma_start(
-                out=out_v[:, q0:q1, :], in_=prod[:, c0:c1].rearrange("p (t h) -> p t h", h=H)
+                out=out_v[:, q0:q1, :], in_=rs[:, c0:c1].rearrange("p (t h) -> p t h", h=H)
             )
 
         def has(t):
@@ -398,11 +396,15 @@ def tile_ryeelman_pa_t_kernel(
             m = k // 2
             inv_now = k % 2 == 0 and 0 <= m < NT // 2
             if has(k + 1):
+                root(k + 1)
+            if k == NT - 2:
+                finish(0, 4)
+            elif has(k + 1):
                 reciprocal(k + 1)
             if has(k - 1):
-                acc[k - 1, 0] = ps_o.tile([P, 512], F32, name="acc_l")
+                acc[k - 1, 1] = ps_o.tile([P, 512], F32, name="acc_r")
             if has(k - 2):
-                add_up(k - 2, acc[k - 1, 0][:, 3 * H : 4 * H], terms_of(k - 2))
+                add_up(k - 2, acc[k - 1, 1][:, 3 * H : 4 * H], terms_of(k - 2))
             if has(k - 1):
                 products(k - 1)
                 if k % 2 == 1:
@@ -411,7 +413,8 @@ def tile_ryeelman_pa_t_kernel(
                 if k % 2 == 1:
                     lin_out(m)
             if k == NT - 1:
-                finish(8, 28)
+                finish(12, 20)
+                finish(20, 28)
             if inv_now:
                 inv_transposes(m)
             if k == -1:
@@ -424,13 +427,12 @@ def tile_ryeelman_pa_t_kernel(
             if inv_now:
                 inv_copy(m)
             if k == NT - 2:
-                finish(0, 8)
+                reciprocal(k + 1)
             if k == NT - 1:
-                scale(k, 0)
-                scale(k, 1)
-                left_times_right(k - 1)
+                for j in range(NJ):
+                    scale(k, j)
                 quantise(k, ((0, 256), (384, 640)))
-                scale(k, 2)
+                left_times_right(k - 1)
                 quantise(k, ((256, 384), (640, 768)))
             elif k == 0:
                 for g in (1, 0):
@@ -441,16 +443,20 @@ def tile_ryeelman_pa_t_kernel(
                     scale(k, j)
             if has(k - 1) and k < NT - 1:
                 left_times_right(k - 1)
-            if inv_now:
+            if inv_now and k > 0:
                 inv_quantise(m)
             if has(k) and k < NT - 1:
                 quantise(k)
+            if k == 0:
+                inv_quantise(m)
             if k == 0:
                 keep_bias()
             if has(k + 2):
                 norm_transposes(k + 2)
             if has(k + 1) and k != -1:
                 raw_transposes(k + 1)
+            if k == NT - 2:
+                finish(4, 12)
             if k < -1 and has(k + 5):
                 load(k + 5)
             if k >= -1 and k % 2 == 1 and has(k + 5):
@@ -467,27 +473,25 @@ def tile_ryeelman_pa_t_kernel(
                 first_channels(k + 4, k + 6)
 
         t = NT - 1
-        slot = t % 3
         left_01 = ps_n.tile([P, 512], F32, name="n_t")
         right_01 = ps_n.tile([P, 512], F32, name="n_t")
         left_2 = ps_e.tile([P, 512], F32, name="eq_t")
         right_2 = ps_e.tile([P, 512], F32, name="eq_t")
         sums = ps_o.tile([P, 512], F32, name="acc_l")
         left_right(t, 0, 2, left_01[:, 0 : 2 * P], right_01[:, 0 : 2 * P])
-        add_up(t - 1, sums[:, H : 2 * H], terms_of(t - 1))
         left_right(t, 2, 3, left_2[:, 0:P], right_2[:, 0:P])
-        nc.scalar.copy(out=rr[:, slot, 0 : 2 * H], in_=right_01[:, 0 : 2 * H])
-        nc.scalar.activation(out=prod[:, 5 * H : 7 * H], in_=prod[:, 5 * H : 7 * H], func=ACT.Tanh)
+        add_up(t - 1, sums[:, H : 2 * H], terms_of(t - 1))
+        nc.scalar.copy(out=rs[:, H : 3 * H], in_=right_01[:, 0 : 2 * H])
         nc.vector.tensor_tensor(
-            out=prod[:, 0 : 2 * H], in0=left_01[:, 0 : 2 * H], in1=rr[:, slot, 0 : 2 * H], op=ALU.mult
+            out=prod[:, t % 3, 0 : 2 * H], in0=left_01[:, 0 : 2 * H], in1=rs[:, H : 3 * H], op=ALU.mult
         )
-        nc.scalar.copy(out=rr[:, slot, 2 * H : 3 * H], in_=right_2[:, 0:H])
+        nc.scalar.copy(out=rs[:, 3 * H : 4 * H], in_=right_2[:, 0:H])
+        nc.scalar.activation(out=rs[:, 5 * H : 7 * H], in_=rs[:, 5 * H : 7 * H], func=ACT.Tanh)
         nc.vector.tensor_tensor(
-            out=prod[:, 2 * H : 3 * H], in0=left_2[:, 0:H], in1=rr[:, slot, 2 * H : 3 * H], op=ALU.mult
+            out=prod[:, t % 3, 2 * H : 3 * H], in0=left_2[:, 0:H], in1=rs[:, 3 * H : 4 * H], op=ALU.mult
         )
-        terms = [lin_b[t // 2][:, P : 2 * P]] + [prod[:, H * j : H * j + H] for j in range(NJ)]
-        add_up(t, sums[:, 0:H], terms)
-        nc.scalar.activation(out=prod[:, 3 * H : 5 * H], in_=sums[:, 0 : 2 * H], func=ACT.Tanh)
+        add_up(t, sums[:, 0:H], terms_of(t))
+        nc.scalar.activation(out=rs[:, 3 * H : 5 * H], in_=sums[:, 0 : 2 * H], func=ACT.Tanh)
         nc.sync.dma_start(
-            out=out_v[:, 0:4, :], in_=prod[:, 3 * H : 7 * H].rearrange("p (t h) -> p t h", h=H)
+            out=out_v[:, 0:4, :], in_=rs[:, 3 * H : 7 * H].rearrange("p (t h) -> p t h", h=H)
         )

@@ -60,6 +60,8 @@ def tile_ryeelman_pa_t_kernel(
         nc.scalar.activation(out=warm[:], in_=one_t[:], func=ACT.Abs_reciprocal_sqrt)
         eps_t = const.tile([P, 1], F32, name="eps_t")
         nc.vector.tensor_scalar(out=eps_t[:], in0=one_t[:], scalar1=EPS, scalar2=None, op0=ALU.mult)
+        zeros = const.tile([P, 512], BF16, name="zeros")
+        nc.vector.memset(zeros[:], 0.0)
         ident = const.tile([P, P], F32, name="ident")
         make_identity(nc, ident[:])
 
@@ -215,8 +217,8 @@ def tile_ryeelman_pa_t_kernel(
                 else:
                     eng.tensor_tensor(out=dst, in0=src, in1=src, op=ALU.mult)
 
-        def norm_transposes(t):
-            for g in (1, 0):
+        def norm_transposes(t, halves=(1, 0)):
+            for g in halves:
                 n_t[t, g] = ps_n.tile([P, 512], F32, name="n_t")
                 for r in range(4):
                     u, e = divmod(r, 2)
@@ -377,9 +379,16 @@ def tile_ryeelman_pa_t_kernel(
                 out=out_v[:, q0:q1, :], in_=rs[:, c0:c1].rearrange("p (t h) -> p t h", h=H)
             )
 
+        spare = ps_o.tile([P, 512], F32, name="acc_r")
+
+        def keep_busy(n):
+            for i in range(n):
+                nc.tensor.matmul(out=spare[:], lhsT=zeros[:, 0:P], rhs=zeros[:], start=True, stop=True)
+
         def has(t):
             return 0 <= t < NT
 
+        keep_busy(5)
         for q0 in (256, 0):
             if q0 == 0:
                 first_channels(0, 1)
@@ -419,6 +428,7 @@ def tile_ryeelman_pa_t_kernel(
                 inv_transposes(m)
             if k == -1:
                 raw_transposes(0)
+                keep_busy(3)
                 transpose_bias()
                 group_weights()
                 quantise_weights()
@@ -451,8 +461,14 @@ def tile_ryeelman_pa_t_kernel(
                 inv_quantise(m)
             if k == 0:
                 keep_bias()
-            if has(k + 2):
+            if k == -2:
+                norm_transposes(0, (1,))
+                keep_busy(2)
+                norm_transposes(0, (0,))
+            elif has(k + 2):
                 norm_transposes(k + 2)
+            if k == -1:
+                keep_busy(5)
             if has(k + 1) and k != -1:
                 raw_transposes(k + 1)
             if k == NT - 2:

from contextlib import ExitStack

import concourse.mybir as mybir
from concourse.masks import make_identity

F32 = mybir.dt.float32
BF16 = mybir.dt.bfloat16
U32 = mybir.dt.uint32
U8 = mybir.dt.uint8
FP8X4 = mybir.dt.float8_e4m3fn_x4
ACT = mybir.ActivationFunctionType
ALU = mybir.AluOpType

P = 128
NT = 32
NJ = 3
CC = 1024
H = 128
EPS = 1e-6
SPLIT = 256
FLOPS = 2 * 4096 * 3 * 1024 * 256 + 2 * 4096 * 512 * 128


def row(t):
    return NT - 1 - t


def tile_ryeelman_pa_t_kernel(
    tc,
    invariant_input,
    equivariant_input,
    invariant_hidden,
    equivariant_hidden,
    W_left,
    W_right,
    W_ii,
    b_ii,
    out,
):
    nc = tc.nc
    hid = equivariant_hidden.rearrange("(p t) j c -> p (t j c)", t=NT)
    out_v = out.rearrange("(p t) h -> p t h", t=NT)
    ii_v = invariant_input.rearrange("(p t) k -> p t k", t=NT)
    ih_v = invariant_hidden.rearrange("(p t) k -> p t k", t=NT)

    with ExitStack() as ctx:
        ctx.enter_context(tc.manual_schedule())
        const = ctx.enter_context(tc.tile_pool(name="const", bufs=1))
        bigp = ctx.enter_context(tc.tile_pool(name="bigp", bufs=3))
        work = ctx.enter_context(tc.tile_pool(name="work", bufs=2))
        work3 = ctx.enter_context(tc.tile_pool(name="work3", bufs=3))
        turns = ctx.enter_context(tc.tile_pool(name="turns", bufs=3))
        ps_n = ctx.enter_context(tc.psum_pool(name="ps_n", bufs=3))
        ps_e = ctx.enter_context(tc.psum_pool(name="ps_e", bufs=3))
        ps_o = ctx.enter_context(tc.psum_pool(name="ps_o", bufs=1))

        one_t = const.tile([P, 1], F32, name="one_t")
        nc.vector.memset(one_t[:], 1.0)
        warm = const.tile([P, 1], F32, name="warm")
        nc.scalar.activation(out=warm[:], in_=one_t[:], func=ACT.Abs_reciprocal_sqrt)
        eps_t = const.tile([P, 1], F32, name="eps_t")
        nc.vector.tensor_scalar(out=eps_t[:], in0=one_t[:], scalar1=EPS, scalar2=None, op0=ALU.mult)
        zeros = const.tile([P, 512], BF16, name="zeros")
        nc.vector.memset(zeros[:], 0.0)
        ident = const.tile([P, P], F32, name="ident")
        make_identity(nc, ident[:])

        pair = {}
        big = {}

        def new_tile(t):
            if t // 2 not in pair:
                pair[t // 2] = bigp.tile([P, 2, NJ, CC], BF16, name="big")
            big[t] = pair[t // 2][:, 1 - t % 2]

        def load_rows(t, j, c0, c1):
            start = (NJ * row(t) + j) * (CC - 1) - 1
            nc.sync.dma_start(out=big[t][:, j, c0:c1], in_=hid[:, start + c0 : start + c1])

        new_tile(0)
        for j in range(NJ):
            load_rows(0, j, 512, CC)
        inp = const.tile([P, NT * NJ], BF16, name="inp")
        nc.sync.dma_start(out=inp[:], in_=equivariant_input.rearrange("(p t) j -> p (t j)", t=NT))
        for j in range(NJ):
            load_rows(0, j, 0, 512)
        last15 = const.tile([P, 16], BF16, name="last15")
        wraw = const.tile([P, 2, 2, 4, H], BF16, name="wraw")
        wiraw = const.tile([P, 4, H], BF16, name="wiraw")
        bias_bf = const.tile([P, H], BF16, name="bias_bf")

        def load_weights():
            for w, weights in ((0, W_left), (1, W_right)):
                nc.sync.dma_start(
                    out=wraw[:, w].rearrange("p g (u e) h -> p (g u) (e h)", u=2),
                    in_=weights.rearrange("(c q e) h -> q c (e h)", c=4, e=2),
                )
            nc.sync.dma_start(
                out=wiraw[:].rearrange("p (u e) h -> p u (e h)", u=2),
                in_=W_ii.rearrange("(u q e) h -> q u (e h)", u=2, e=2),
            )
            nc.sync.dma_start(out=bias_bf[:], in_=b_ii.partition_broadcast(P))

        inv_all = const.tile([P, NT, 512], BF16, name="inv_all")
        icodes = const.tile([P, NT * P], U32, name="icodes", align_bytes=64)
        iscl = const.tile([P, NT * P], U8, name="iscl", align_bytes=64)
        rs = const.tile([P, 3 * H + NT * H], F32, name="rs")
        prod = const.tile([P, 3, 3 * H], F32, name="prod")
        bias_f = const.tile([P, H], F32, name="bias_f")
        bias_t = const.tile([P, 1], F32, name="bias_t")

        wgrp = const.tile([P, 2, 2 * H, 4], BF16, name="wgrp", align_bytes=64)
        wcodes = const.tile([P, 2 * 2 * H], U32, name="wcodes", align_bytes=64)
        wscl = const.tile([P, 2 * 2 * H], U8, name="wscl", align_bytes=64)
        wigrp = const.tile([P, H, 4], BF16, name="wigrp", align_bytes=64)
        wicodes = const.tile([P, H], U32, name="wicodes", align_bytes=64)
        wiscl = const.tile([P, H], U8, name="wiscl", align_bytes=64)

        def group_weights():
            for g in range(2):
                nc.vector.tensor_copy(
                    out=wgrp[:, g].rearrange("p (w h) t -> p w h t", w=2),
                    in_=wraw[:, :, g].rearrange("p w t h -> p w h t"),
                )
            nc.vector.tensor_copy(out=wigrp[:], in_=wiraw[:].rearrange("p t h -> p h t"))

        def quantise_weights():
            nc.vector.quantize_mx(
                out=wcodes[:].bitcast(FP8X4),
                scales=wscl[:],
                in_=wgrp[:].rearrange("p g c t -> p (g c t)"),
            )
            nc.vector.quantize_mx(
                out=wicodes[:].bitcast(FP8X4),
                scales=wiscl[:],
                in_=wigrp[:].rearrange("p h t -> p (h t)"),
            )

        def transpose_bias():
            nc.vector.tensor_copy(out=bias_f[:], in_=bias_bf[:])
            acc[-1, 0] = ps_o.tile([P, 512], F32, name="acc_l")
            nc.tensor.transpose(out=acc[-1, 0][:, 0:P], in_=bias_f[:], identity=ident[:])

        def keep_bias():
            nc.vector.tensor_copy(out=bias_t[:], in_=acc[-1, 0][:, 0:1])

        sq = {}
        n_t = {}
        n2 = {}
        recip = {}
        eq_t = {}
        grp = {}
        codes = {}
        scl = {}
        acc = {}
        inv_ps = {}
        inv_g = {}
        lin_b = {}

        def load_two_rows(i, s0, s1):
            start = (NJ * row(2 * i + 1) + s0) * (CC - 1) - 1
            n = (s1 - s0) // 2
            nc.sync.dma_start(
                out=pair[i][:].rearrange("p t j c -> p (t j) c")[:, s0 : min(s1, 6) : 2, :],
                in_=hid[:, start : start + 2 * n * (CC - 1)].rearrange("p (i s) -> p i s", i=n)[:, :, 0:CC],
            )

        def load(t):
            new_tile(t)
            s = NJ * (1 - t % 2)
            load_two_rows(t // 2, s, s + 4)
            load_rows(t, 1, 0, CC)

        def load_pair(i):
            new_tile(2 * i)
            new_tile(2 * i + 1)
            if i < NT // 2 - 1:
                load_two_rows(i, 0, 6)
            else:
                nc.sync.dma_start(out=last15[:, 0:15], in_=hid[:, 0:15])
                load_rows(2 * i + 1, 0, 16, CC)
                load_two_rows(i, 2, 6)
            load_two_rows(i, 1, 7)

        def first_channels(t0, t1):
            n, q = t1 - t0, row(t1 - 1)
            s = 0 if n == 2 else 1 - t0 % 2
            nc.scalar.copy(
                out=pair[t0 // 2][:, s : s + n, :, 0:1],
                in_=inp[:, NJ * q : NJ * q + n * NJ].rearrange("p (t j c) -> p t j c", j=NJ, c=1),
            )
            if t1 == NT:
                nc.scalar.copy(out=big[NT - 1][:, 0, 1:16], in_=last15[:, 0:15])

        def load_inv(t0, t1):
            ts = slice(row(t1 - 1), row(t0) + 1)
            nc.sync.dma_start(out=inv_all[:, ts, 0:384], in_=ii_v[:, ts, :])
            nc.sync.dma_start(out=inv_all[:, ts, 384:512], in_=ih_v[:, ts, :])

        def squares(t, plan=None):
            if t not in sq:
                sq[t] = (
                    work.tile([P, NJ, 2, SPLIT], F32, name="sq"),
                    turns.tile([P, NJ, 2, 512 - SPLIT], F32, name="turn", align_bytes=64),
                )
            if plan is None:
                plan = (
                    (nc.scalar, 0, 3, 0, SPLIT),
                    (nc.vector if t < 3 else nc.gpsimd, 0, 3, SPLIT, 512),
                )
            for eng, j0, j1, q0, q1 in plan:
                src = big[t][:, j0:j1, 2 * q0 : 2 * q1].rearrange("p j (q e) -> p j e q", e=2)
                h, o = (0, 0) if q0 < SPLIT else (1, SPLIT)
                dst = sq[t][h][:, j0:j1, :, q0 - o : q1 - o]
                if eng is nc.scalar:
                    nc.scalar.activation(out=dst, in_=src, func=ACT.Square)
                else:
                    eng.tensor_tensor(out=dst, in0=src, in1=src, op=ALU.mult)

        def norm_transposes(t, halves=(1, 0)):
            for g in halves:
                n_t[t, g] = ps_n.tile([P, 512], F32, name="n_t")
                for r in range(4):
                    u, e = divmod(r, 2)
                    for j in range(NJ):
                        nc.tensor.matmul(
                            out=n_t[t, g][:, P * r : P * r + P],
                            lhsT=sq[t][g][:, j, e, P * u : P * u + P],
                            rhs=ident[:],
                            is_transpose=True,
                            start=(j == 0),
                            stop=(j == 2),
                        )

        def root(t):
            n2[t] = work.tile([P, CC], F32, name="n2")
            for g in (1, 0):
                nc.scalar.activation(
                    out=n2[t][:, 512 * g : 512 * g + 512].rearrange("p (b r) -> p b r", r=4),
                    in_=n_t[t, g][:].rearrange("p (r b) -> p b r", r=4),
                    func=ACT.Abs_reciprocal_sqrt,
                    bias=eps_t[:, 0:1],
                )

        def reciprocal(t):
            recip[t] = work3.tile([P, CC], F32, name="recip")
            for c0, c1 in ((512, CC), (0, 512)):
                nc.scalar.activation(out=recip[t][:, c0:c1], in_=n2[t][:, c0:c1], func=ACT.Square)

        def raw_transposes(t):
            words = big[t][:].bitcast(F32)
            for j in range(NJ):
                eq_t[t, j] = ps_e.tile([P, 512], F32, name="eq_t")
                for g in range(2):
                    for u in range(2):
                        nc.tensor.transpose(
                            out=eq_t[t, j][:, P * (2 * u + g) : P * (2 * u + g) + P],
                            in_=words[:, j, P * (2 * g + u) : P * (2 * g + u) + P],
                            identity=ident[:],
                        )

        def scale(t, j, g0=0, g1=2):
            if t not in grp:
                grp[t] = turns.tile([P, 2, NJ, 512], BF16, name="turn", align_bytes=64)
            nc.vector.tensor_tensor(
                out=grp[t][:, g0:g1, j, :].rearrange("p g (b u e) -> p g b u e", u=2, e=2),
                in0=eq_t[t, j][:].bitcast(BF16).rearrange("p (u g b e) -> p g b u e", u=2, g=2, e=2)[:, g0:g1],
                in1=recip[t][:].rearrange("p (g b u e) -> p g b u e", g=2, u=2, e=2)[:, g0:g1],
                op=ALU.mult,
            )

        def quantise(t, pieces=((0, 512), (512, 768))):
            if t not in codes:
                codes[t] = work3.tile([P, NJ * 256], U32, name="codes", align_bytes=64)
                scl[t] = work3.tile([P, NJ * 256], U8, name="scl", align_bytes=64)
            flat = grp[t][:].rearrange("p g j c -> p (g j c)")
            for w0, w1 in pieces:
                nc.vector.quantize_mx(
                    out=codes[t][:, w0:w1].bitcast(FP8X4),
                    scales=scl[t][:, w0:w1],
                    in_=flat[:, 4 * w0 : 4 * w1],
                )

        def inv_transposes(m):
            inv_ps[m] = ps_n.tile([P, 512], F32, name="n_t")
            for tt in range(2):
                words = inv_all[:, row(2 * m + tt), :].bitcast(F32)
                for u in range(2):
                    nc.tensor.transpose(
                        out=inv_ps[m][:, P * (2 * u + tt) : P * (2 * u + tt) + P],
                        in_=words[:, P * u : P * u + P],
                        identity=ident[:],
                    )

        def inv_copy(m):
            inv_g[m] = work.tile([P, 2 * P * 4], BF16, name="inv_g", align_bytes=64)
            nc.scalar.copy(
                out=inv_g[m][:].bitcast(F32).rearrange("p (x u) -> p x u", u=2),
                in_=inv_ps[m][:].rearrange("p (u x) -> p x u", u=2),
            )

        def inv_quantise(m):
            cols = slice(256 * m, 256 * m + 256)
            nc.vector.quantize_mx(
                out=icodes[:, cols].bitcast(FP8X4), scales=iscl[:, cols], in_=inv_g[m][:]
            )

        def left_right(t, j0, j1, left, right):
            for g in range(2):
                rows = slice(384 * g + P * j0, 384 * g + P * j1)
                for w, dst in ((0, left), (1, right)):
                    wc = slice(256 * g + P * w, 256 * g + P * w + P)
                    nc.tensor.matmul_mx(
                        out=dst,
                        lhsT=wcodes[:, wc].bitcast(FP8X4),
                        lhsT_scale=wscl[:, wc],
                        rhs=codes[t][:, rows].bitcast(FP8X4),
                        rhs_scale=scl[t][:, rows],
                        start=(g == 0),
                        stop=(g == 1),
                    )

        def lin(m):
            cols = slice(2 * P * m, 2 * P * m + 2 * P)
            inv_ps[m] = ps_n.tile([P, 512], F32, name="n_t")
            nc.tensor.matmul_mx(
                out=inv_ps[m][:, 0 : 2 * P],
                lhsT=wicodes[:].bitcast(FP8X4),
                lhsT_scale=wiscl[:],
                rhs=icodes[:, cols].bitcast(FP8X4),
                rhs_scale=iscl[:, cols],
                start=True,
                stop=True,
            )

        def lin_out(m):
            lin_b[m] = work3.tile([P, 2 * P], F32, name="lin_b")
            nc.scalar.activation(
                out=lin_b[m][:], in_=inv_ps[m][:, 0 : 2 * P], func=ACT.Identity, bias=bias_t[:, 0:1]
            )

        def products(t):
            acc[t, 0] = ps_o.tile([P, 512], F32, name="acc_l")
            for j0, j1 in ((0, 2), (2, 3)):
                left_right(t, j0, j1, acc[t, 0][:, P * j0 : P * j1], acc[t, 1][:, P * j0 : P * j1])

        def add_up(t, dst, terms):
            for i, term in enumerate(terms):
                nc.tensor.matmul(
                    out=dst,
                    lhsT=term,
                    rhs=ident[:],
                    is_transpose=True,
                    start=(i == 0),
                    stop=(i == len(terms) - 1),
                )

        def terms_of(t):
            return [lin_b[t // 2][:, P * (t % 2) : P * (t % 2) + P]] + [
                prod[:, t % 3, H * j : H * j + H] for j in range(NJ)
            ]

        def right_out(t):
            n = 4 * H if t > 0 else 3 * H
            base = H * (NT - t)
            nc.scalar.copy(out=rs[:, base : base + n], in_=acc[t, 1][:, 0:n])

        def left_times_right(t):
            base = H * (NT - t)
            nc.vector.tensor_tensor(
                out=prod[:, t % 3, :], in0=acc[t, 0][:, 0 : 3 * H], in1=rs[:, base : base + 3 * H], op=ALU.mult
            )

        def finish(t0, t1):
            q0, q1 = row(t1 - 1), row(t0) + 1
            c0, c1 = 3 * H + H * q0, 3 * H + H * q1
            nc.scalar.activation(out=rs[:, c0:c1], in_=rs[:, c0:c1], func=ACT.Tanh)
            nc.sync.dma_start(
                out=out_v[:, q0:q1, :], in_=rs[:, c0:c1].rearrange("p (t h) -> p t h", h=H)
            )

        spare = ps_o.tile([P, 512], F32, name="acc_r")

        def keep_busy(n):
            for i in range(n):
                nc.tensor.matmul(out=spare[:], lhsT=zeros[:, 0:P], rhs=zeros[:], start=True, stop=True)

        def has(t):
            return 0 <= t < NT

        keep_busy(5)
        for q0 in (256, 0):
            if q0 == 0:
                first_channels(0, 1)
            plan = (
                (nc.scalar, 0, 1, q0, q0 + 256),
                (nc.vector, 1, 2, q0, q0 + 256),
                (nc.scalar, 2, 3, q0, q0 + 128),
                (nc.vector, 2, 3, q0 + 128, q0 + 256),
            )
            squares(0, plan)

        inv_loads = {-2: (0, 4), 0: (4, 8), 2: (8, 16), 5: (16, 24), 8: (24, 32)}
        for k in range(-4, NT):
            m = k // 2
            inv_now = k % 2 == 0 and 0 <= m < NT // 2
            if has(k + 1):
                root(k + 1)
            if k == NT - 2:
                finish(0, 4)
            elif has(k + 1):
                reciprocal(k + 1)
            if has(k - 1):
                acc[k - 1, 1] = ps_o.tile([P, 512], F32, name="acc_r")
            if has(k - 2):
                add_up(k - 2, acc[k - 1, 1][:, 3 * H : 4 * H], terms_of(k - 2))
            if has(k - 1):
                products(k - 1)
                if k % 2 == 1:
                    lin(m)
                right_out(k - 1)
                if k % 2 == 1:
                    lin_out(m)
            if k == NT - 1:
                finish(12, 20)
                finish(20, 28)
            if inv_now:
                inv_transposes(m)
            if k == -1:
                raw_transposes(0)
                keep_busy(3)
                transpose_bias()
                group_weights()
                quantise_weights()
                first_channels(2, 3)
                squares(2)
            if inv_now:
                inv_copy(m)
            if k == NT - 2:
                reciprocal(k + 1)
            if k == NT - 1:
                for j in range(NJ):
                    scale(k, j)
                quantise(k, ((0, 256), (384, 640)))
                left_times_right(k - 1)
                quantise(k, ((256, 384), (640, 768)))
            elif k == 0:
                for g in (1, 0):
                    for j in range(NJ):
                        scale(k, j, g, g + 1)
            elif has(k):
                for j in range(NJ):
                    scale(k, j)
            if has(k - 1) and k < NT - 1:
                left_times_right(k - 1)
            if inv_now and k > 0:
                inv_quantise(m)
            if has(k) and k < NT - 1:
                quantise(k)
            if k == 0:
                inv_quantise(m)
            if k == 0:
                keep_bias()
            if k == -2:
                norm_transposes(0, (1,))
                keep_busy(2)
                norm_transposes(0, (0,))
            elif has(k + 2):
                norm_transposes(k + 2)
            if k == -1:
                keep_busy(5)
            if has(k + 1) and k != -1:
                raw_transposes(k + 1)
            if k == NT - 2:
                finish(4, 12)
            if k < -1 and has(k + 5):
                load(k + 5)
            if k >= -1 and k % 2 == 1 and has(k + 5):
                load_pair((k + 5) // 2)
            if k == -4:
                load_weights()
            if k in inv_loads:
                load_inv(*inv_loads[k])
            if has(k + 3) and k not in (-3, -1):
                if k < 1:
                    first_channels(k + 3, k + 4)
                squares(k + 3)
            if has(k + 4) and k % 2 == 0 and k >= 0:
                first_channels(k + 4, k + 6)

        t = NT - 1
        left_01 = ps_n.tile([P, 512], F32, name="n_t")
        right_01 = ps_n.tile([P, 512], F32, name="n_t")
        left_2 = ps_e.tile([P, 512], F32, name="eq_t")
        right_2 = ps_e.tile([P, 512], F32, name="eq_t")
        sums = ps_o.tile([P, 512], F32, name="acc_l")
        left_right(t, 0, 2, left_01[:, 0 : 2 * P], right_01[:, 0 : 2 * P])
        left_right(t, 2, 3, left_2[:, 0:P], right_2[:, 0:P])
        add_up(t - 1, sums[:, H : 2 * H], terms_of(t - 1))
        nc.scalar.copy(out=rs[:, H : 3 * H], in_=right_01[:, 0 : 2 * H])
        nc.vector.tensor_tensor(
            out=prod[:, t % 3, 0 : 2 * H], in0=left_01[:, 0 : 2 * H], in1=rs[:, H : 3 * H], op=ALU.mult
        )
        nc.scalar.copy(out=rs[:, 3 * H : 4 * H], in_=right_2[:, 0:H])
        nc.scalar.activation(out=rs[:, 5 * H : 7 * H], in_=rs[:, 5 * H : 7 * H], func=ACT.Tanh)
        nc.vector.tensor_tensor(
            out=prod[:, t % 3, 2 * H : 3 * H], in0=left_2[:, 0:H], in1=rs[:, 3 * H : 4 * H], op=ALU.mult
        )
        add_up(t, sums[:, 0:H], terms_of(t))
        nc.scalar.activation(out=rs[:, 3 * H : 5 * H], in_=sums[:, 0 : 2 * H], func=ACT.Tanh)
        nc.sync.dma_start(
            out=out_v[:, 0:4, :], in_=rs[:, 3 * H : 7 * H].rearrange("p (t h) -> p t h", h=H)
        )
